import numpy as np
import ml_dtypes


def mxq(x, axis, fmt="e4m3"):
    dtype, down = {"e4m3": (ml_dtypes.float8_e4m3fn, 7), "e5m2": (ml_dtypes.float8_e5m2, 14)}[fmt]
    v = np.moveaxis(np.asarray(x, np.float32).astype(ml_dtypes.bfloat16).astype(np.float64), axis, -1)
    blocks = v.reshape(v.shape[:-1] + (-1, 32))
    amax = np.abs(blocks).max(-1, keepdims=True)
    byte = np.maximum(np.where(amax > 0, np.frexp(amax)[1] - 1 + 127, 0) - down, 1)
    scale = np.exp2(byte - 127.0)
    codes = (blocks / scale).astype(np.float32).astype(dtype).astype(np.float64)
    return np.moveaxis((codes * scale).reshape(v.shape), -1, axis)


WIDE = False


def mx_kscale(k):
    if not WIDE:
        return np.ones(k)
    levels = np.array([10, -10, 5, -5, 0])
    if k % 512:
        return np.exp2(np.random.permutation(np.resize(levels, k // 32))).repeat(32)
    a = np.empty((k // 512, 16))
    for p in range(k // 512):
        a[p, :8] = np.random.permutation(np.resize(levels, 8))
        for g in range(8):
            far = levels[np.abs(levels - a[p, g]) >= 10]
            a[p, g + 8] = far[np.random.randint(len(far))]
    return np.exp2(a.ravel()).repeat(32)


BF16 = ml_dtypes.bfloat16


def bf(x):
    return np.asarray(x, np.float32).astype(BF16)


def f64(x):
    return np.asarray(x).astype(np.float64)


B, S, DIM, KV, H = 4, 128, 2048, 512, 16
HD = DIM // H
G = 0.6 * DIM ** 0.25


def heads(v):
    return v.reshape(B, S, H, HD).transpose(0, 2, 1, 3)


def rope(v, cos, sin):
    vr, vi = v[..., 0::2], v[..., 1::2]
    return np.stack([vr * cos - vi * sin, vr * sin + vi * cos], axis=-1).reshape(v.shape)


def draw0():
    s, u = mx_kscale(DIM), mx_kscale(KV)
    ang = np.outer(np.arange(S), 1.0 / 10000.0 ** (np.arange(0, HD, 2) / HD))
    return {"x": bf(np.random.standard_normal((B, S, DIM)) * s),
            "rope_cos": bf(np.cos(ang)),
            "rope_sin": bf(np.sin(ang)),
            "W_kv_down": bf(np.random.standard_normal((KV, DIM)) / np.sqrt(DIM) * u[:, None] / s),
            "b_kv_down": bf(np.random.standard_normal(KV) * 0.3 * u),
            "Wq": bf(np.random.standard_normal((DIM, DIM)) * G / np.sqrt(DIM) / s),
            "bq": bf(np.random.standard_normal(DIM) * 0.2 * G),
            "W_uk": bf(np.random.standard_normal((DIM, KV)) * G / np.sqrt(KV) / u),
            "b_uk": bf(np.random.standard_normal(DIM) * 0.2 * G)}


def core(x, rope_cos, rope_sin, W_kv_down, b_kv_down, Wq, bq, W_uk, b_uk):
    cos, sin = f64(rope_cos), f64(rope_sin)
    xq = mxq(f64(x), 2, "e4m3")
    l_kv = (xq @ mxq(f64(W_kv_down), 1, "e4m3").T) + f64(b_kv_down)
    q = (xq @ mxq(f64(Wq), 1, "e4m3").T) + f64(bq)
    k = (mxq(l_kv, 2, "e4m3") @ mxq(f64(W_uk), 1, "e4m3").T) + f64(b_uk)
    q_rot = rope(heads(q), cos, sin)
    k_rot = rope(heads(k), cos, sin)
    z = q_rot * k_rot * DIM ** (-0.5)
    e = np.exp(z - z.max(-1, keepdims=True))
    return e / e.sum(-1, keepdims=True)


def e4m3fn_bytes(y):
    return np.clip(np.asarray(y, np.float64), -448.0, 448.0).astype(np.float32).astype(ml_dtypes.float8_e4m3fn).view(np.uint8)


def e4m3fn_values(b):
    return np.asarray(b, np.uint8).view(ml_dtypes.float8_e4m3fn).astype(np.float64)


def setup_inputs():
    d = draw0()
    x0 = np.asarray(d['Wq']).astype(np.float64)
    s = (np.max(np.abs(x0), axis=(0,), keepdims=True) / 448.0).astype(np.float32)
    out = {}
    for k, v in d.items():
        if k == 'Wq':
            out['Wq_bytes'] = e4m3fn_bytes(x0 / s.astype(np.float64))
            out['Wq_scale'] = s
        else:
            out[k] = v
    return out


def reference(x, rope_cos, rope_sin, W_kv_down, b_kv_down, Wq_bytes, Wq_scale, bq, W_uk, b_uk):
    return core(x, rope_cos, rope_sin, W_kv_down, b_kv_down, e4m3fn_values(Wq_bytes) * Wq_scale.astype(np.float64), bq, W_uk, b_uk)

@@ -1,0 +1,597 @@
+from contextlib import ExitStack
+
+import concourse.mybir as mybir
+from concourse.masks import make_identity
+
+F32 = mybir.dt.float32
+BF16 = mybir.dt.bfloat16
+U32 = mybir.dt.uint32
+U8 = mybir.dt.uint8
+FP8 = mybir.dt.float8_e4m3fn
+FP8X4 = mybir.dt.float8_e4m3fn_x4
+ALU = mybir.AluOpType
+ACT = mybir.ActivationFunctionType
+AX = mybir.AxisListType
+
+B, S, DIM, KV, H = 4, 128, 2048, 512, 16
+HD = DIM // H
+PAIRS = HD // 2
+T = B * S
+P = 128
+G = DIM // 512
+J = H // 2
+KAPPA = DIM ** -0.5
+
+FLOPS = 2 * T * (DIM * KV + DIM * DIM + KV * DIM)
+
+
+def tile_multilatentattention_pa_kernel(
+    tc, x, rope_cos, rope_sin, W_kv_down, b_kv_down, Wq_bytes, Wq_scale, bq, W_uk, b_uk, out
+):
+    nc = tc.nc
+    with ExitStack() as ctx:
+        ctx.enter_context(tc.manual_schedule())
+        keep = ctx.enter_context(tc.tile_pool(name="keep", bufs=1))
+        work = ctx.enter_context(tc.tile_pool(name="work", bufs=2))
+        psum = ctx.enter_context(tc.psum_pool(name="psum", bufs=1))
+
+        ident = keep.tile([P, P], F32, name="ident")
+        make_identity(nc, ident[:])
+        warm = keep.tile([P, 1], F32, name="warm")
+        nc.vector.memset(warm[:], 0.0)
+        nc.scalar.activation(out=warm[:], in_=warm[:], func=ACT.Exp)
+        cs_raw = keep.tile([P, 2, 2, PAIRS], BF16, name="cs_raw")
+        sc = keep.tile([P, G * 4], F32, name="sc")
+        for h in range(2):
+            nc.sync.dma_start(out=cs_raw[:, 0, h, :], in_=rope_cos)
+            nc.sync.dma_start(out=cs_raw[:, 1, h, :], in_=rope_sin)
+        nc.sync.dma_start(
+            out=sc[:].rearrange("p (g t) -> p g t", t=4),
+            in_=Wq_scale.rearrange("o (g p t) -> p (o g) t", p=P, t=4),
+        )
+        raws = {}
+        byts = {}
+
+        def load_x(b):
+            raw = work.tile([P, DIM], BF16, name="raw", bufs=8)
+            nc.sync.dma_start(out=raw[:], in_=x[b])
+            raws["x", b] = raw
+
+        def load_wd(t):
+            raw = work.tile([P, DIM], BF16, name="raw", bufs=8)
+            nc.sync.dma_start(out=raw[:], in_=W_kv_down.rearrange("(m t) k -> t m k", t=4)[t])
+            raws["d", t] = raw
+
+        def load_wuk(jj):
+            raw = work.tile([P, DIM], BF16, name="raw", bufs=8)
+            nc.sync.dma_start(
+                out=raw[:].rearrange("p (j c) -> p j c", j=2),
+                in_=W_uk.rearrange("(j p e) k -> p j (e k)", p=P, e=2)[:, 2 * jj : 2 * jj + 2, :],
+            )
+            raws["u", jj] = raw
+
+        def load_wq(j, halves=1):
+            byt = keep.tile([P, 2, DIM], U8, name="wq_bytes_%d" % j)
+            byts[j] = byt
+            return byt
+
+        def load_wq_part(j, c):
+            nc.sync.dma_start(
+                out=byts[j][:, :, c],
+                in_=Wq_bytes.rearrange("(j p e) k -> j p e k", p=P, e=2)[j][:, :, c],
+            )
+
+        full = slice(0, DIM)
+        for j in range(J):
+            load_wq(j)
+        load_wq_part(0, slice(0, DIM // 2))
+        load_x(0)
+        load_wq_part(0, slice(DIM // 2, DIM))
+        load_x(1)
+        load_x(2)
+        load_x(3)
+        load_wq_part(1, full)
+        load_wd(0)
+        load_wd(1)
+        load_wd(2)
+        load_wd(3)
+        load_wq_part(2, full)
+        load_wuk(0)
+        load_wq_part(3, full)
+        load_wuk(1)
+        load_wq_part(4, full)
+        load_wq_part(5, full)
+        load_wuk(2)
+        load_wq_part(6, full)
+        load_wq_part(7, full)
+        load_wuk(3)
+
+        bd_raw = keep.tile([P, 4], BF16, name="bd_raw")
+        nc.gpsimd.dma_start(out=bd_raw[:], in_=b_kv_down.rearrange("(p t) -> p t", t=4))
+        bqk_raw = keep.tile([P, 2, J, 2], BF16, name="bqk_raw")
+        nc.gpsimd.dma_start(out=bqk_raw[:, 0], in_=bq.rearrange("(j p e) -> p j e", p=P, e=2))
+        nc.gpsimd.dma_start(out=bqk_raw[:, 1], in_=b_uk.rearrange("(j p e) -> p j e", p=P, e=2))
+
+        csf = keep.tile([P, 2, P], F32, name="csf")
+        nc.vector.tensor_copy(out=csf[:], in_=cs_raw[:].rearrange("p a h i -> p a (h i)"))
+        tabs_ps = psum.tile([P, 2, P], F32, name="tabs_ps", tag="z", bufs=2)
+        for a in range(2):
+            nc.tensor.transpose(tabs_ps[:, a, :], csf[:, a, :], ident[:])
+        tk = keep.tile([P, 2, P], F32, name="tk")
+        nc.vector.tensor_copy(out=tk[:], in_=tabs_ps[:])
+        tq = keep.tile([P, 2, P], F32, name="tq")
+        nc.vector.tensor_scalar(out=tq[:], in0=tk[:], scalar1=-KAPPA, scalar2=None, op0=ALU.mult)
+        rr = keep.tile([P, 2, P], F32, name="rr")
+        nc.vector.tensor_tensor(out=rr[:], in0=tk[:], in1=tq[:], op=ALU.mult)
+        rho = keep.tile([P, P], F32, name="rho")
+        nc.vector.tensor_tensor(out=rho[:], in0=rr[:, 0, :], in1=rr[:, 1, :], op=ALU.add)
+        bd = keep.tile([P, 4], F32, name="bd")
+        bqk = keep.tile([P, 2, J, 2], F32, name="bqk")
+
+        def biases():
+            nc.vector.tensor_copy(out=bd[:], in_=bd_raw[:])
+            nc.vector.tensor_copy(out=bqk[:], in_=bqk_raw[:])
+
+        def bc(tab):
+            return tab.unsqueeze(1).to_broadcast([P, B, S])
+
+        def b3(ap):
+            return ap.rearrange("p (b s) -> p b s", b=B)
+
+        xw = keep.tile([P, G, T], U32, name="xw", align_bytes=64)
+        xs = keep.tile([P, G, T], U8, name="xs", align_bytes=64)
+        dw = keep.tile([P, G, KV], U32, name="dw", align_bytes=64)
+        ds = keep.tile([P, G, KV], U8, name="ds", align_bytes=64)
+        grps = {}
+
+        def copy_out(eng, out_ap, in_ap):
+            if eng == "v":
+                nc.vector.tensor_copy(out=out_ap, in_=in_ap)
+            else:
+                nc.scalar.copy(out_ap, in_ap)
+
+        rbank = {}
+
+        def rows_tr(kind, b, gg):
+            words = raws[kind, b][:].bitcast(F32)
+            bank = psum.tile([P, 2, 2, P], F32, name="bank", tag="w", bufs=3)
+            for g2 in range(2):
+                g = 2 * gg + g2
+                for u in range(2):
+                    nc.tensor.transpose(
+                        bank[:, g2, u, :], words[:, 256 * g + u : 256 * (g + 1) : 2], ident[:]
+                    )
+            rbank[kind, b, gg] = bank
+
+        def rows_out(kind, b, gg, eng):
+            if kind not in grps:
+                grp = work.tile([P, G, T, 4], BF16, name="grp2048", bufs=1, align_bytes=64)
+                grps[kind] = grp
+            dst = grps[kind][:, 2 * gg : 2 * gg + 2, P * b : P * (b + 1), :]
+            copy_out(
+                eng,
+                dst.rearrange("p g n t -> p g (n t)").bitcast(F32).rearrange("p g (n u) -> p g n u", u=2),
+                rbank[kind, b, gg][:].rearrange("p g u n -> p g n u"),
+            )
+
+        def rows_quant(kind, g, words, scales):
+            nc.vector.quantize_mx(
+                out=words[:, g, :].bitcast(FP8X4),
+                scales=scales[:, g, :],
+                in_=grps[kind][:, g].rearrange("p n t -> p (n t)"),
+            )
+
+        wides = {}
+        wqg = {}
+        wqw = {}
+
+        def wq_widen(j, half, e):
+            if j not in wides:
+                wide = work.tile([P, 2, DIM], BF16, name="wide", bufs=2)
+                wides[j] = wide
+            c = slice(1024 * half, 1024 * (half + 1))
+            nc.scalar.copy(wides[j][:, e, c], byts[j][:, e, c].bitcast(FP8))
+
+        wbank = {}
+
+        def wq_tr(j, g):
+            bank = psum.tile([P, 2, 256], F32, name="wbank", tag="w", bufs=3)
+            for e in range(2):
+                words = wides[j][:, e, :].bitcast(F32)
+                for u in range(2):
+                    nc.tensor.transpose(
+                        bank[:, u, P * e : P * (e + 1)],
+                        words[:, 256 * g + u : 256 * (g + 1) : 2],
+                        ident[:],
+                    )
+            wbank[j, g] = bank
+
+        def wq_scale(j, g):
+            if j not in wqg:
+                grp = work.tile([P, G, 256 * 4], BF16, name="wqgrp", bufs=2, align_bytes=64)
+                wqg[j] = grp
+            nc.vector.tensor_tensor(
+                out=wqg[j][:, g, :].rearrange("p (n u e) -> p n u e", u=2, e=2),
+                in0=wbank[j, g][:].bitcast(BF16).rearrange("p u (n e) -> p n u e", e=2),
+                in1=sc[:, 4 * g : 4 * g + 4]
+                .rearrange("p (u e) -> p u e", e=2)
+                .unsqueeze(1)
+                .to_broadcast([P, 256, 2, 2]),
+                op=ALU.mult,
+            )
+
+        def wq_quant(j):
+            wcode = work.tile([P, G * 256], U32, name="wqcode", bufs=3, align_bytes=64)
+            wscal = work.tile([P, G * 256], U8, name="wqscal", bufs=3, align_bytes=64)
+            nc.vector.quantize_mx(
+                out=wcode[:].bitcast(FP8X4),
+                scales=wscal[:],
+                in_=wqg[j][:].rearrange("p g c -> p (g c)"),
+            )
+            wqw[j] = (wcode, wscal)
+
+        uw = keep.tile([P, J, 2, P], U32, name="uw", align_bytes=64)
+        us = keep.tile([P, J, 2, P], U8, name="us", align_bytes=64)
+
+        ubank = {}
+        ugs = {}
+
+        def wuk_tr(j):
+            bank = psum.tile([P, 2, 2, P], F32, name="ubank", tag="w", bufs=3)
+            words = raws["u", j // 2][:].bitcast(F32).rearrange("p (j e w) -> p j e w", j=2, e=2)
+            for e in range(2):
+                for u in range(2):
+                    nc.tensor.transpose(bank[:, e, u, :], words[:, j % 2, e, u:256:2], ident[:])
+            ubank[j] = bank
+
+        def wuk_out(j, eng):
+            ug = work.tile([P, 2, P, 4], BF16, name="ug", bufs=2, align_bytes=64)
+            copy_out(
+                eng,
+                ug[:].rearrange("p e n t -> p e (n t)").bitcast(F32).rearrange("p e (n u) -> p e n u", u=2),
+                ubank[j][:].rearrange("p e u n -> p e n u"),
+            )
+            ugs[j] = ug
+
+        def wuk_quant(j):
+            nc.vector.quantize_mx(
+                out=uw[:, j].rearrange("p e n -> p (e n)").bitcast(FP8X4),
+                scales=us[:, j].rearrange("p e n -> p (e n)"),
+                in_=ugs[j][:].rearrange("p e n t -> p (e n t)"),
+            )
+
+        lg = keep.tile([P, T, 4], BF16, name="lg", align_bytes=64)
+        lw = keep.tile([P, T], U32, name="lw", align_bytes=64)
+        ls = keep.tile([P, T], U8, name="ls", align_bytes=64)
+
+        lbank = {}
+
+        def lkv_mm(b):
+            bank = psum.tile([P, 4, P], F32, name="lbank", tag="q", bufs=2)
+            for t in range(4):
+                for g in range(G):
+                    nc.tensor.matmul_mx(
+                        out=bank[:, t, :],
+                        lhsT=dw[:, g, P * t : P * (t + 1)].bitcast(FP8X4),
+                        lhsT_scale=ds[:, g, P * t : P * (t + 1)],
+                        rhs=xw[:, g, P * b : P * (b + 1)].bitcast(FP8X4),
+                        rhs_scale=xs[:, g, P * b : P * (b + 1)],
+                        start=(g == 0),
+                        stop=(g == G - 1),
+                    )
+            lbank[b] = bank
+
+        def lkv_out(b):
+            nc.vector.tensor_tensor(
+                out=lg[:, P * b : P * (b + 1), :],
+                in0=lbank[b][:].rearrange("p t n -> p n t"),
+                in1=bd[:].unsqueeze(1).to_broadcast([P, P, 4]),
+                op=ALU.add,
+            )
+
+        def lkv_quant():
+            nc.vector.quantize_mx(
+                out=lw[:].bitcast(FP8X4), scales=ls[:], in_=lg[:].rearrange("p n t -> p (n t)")
+            )
+
+        kbank = {}
+        kts = {}
+        qbank = {}
+        qts = {}
+        pts = {}
+        kcs = {}
+        zes = {}
+        zos = {}
+        zbank = {}
+        nms = {}
+        sms = {}
+        ets = {}
+
+        def k_mm(j, e):
+            kb = psum.tile([P, T], F32, name="kb", tag="k", bufs=1)
+            nc.tensor.matmul_mx(
+                out=kb[:],
+                lhsT=uw[:, j, e, :].bitcast(FP8X4),
+                lhsT_scale=us[:, j, e, :],
+                rhs=lw[:].bitcast(FP8X4),
+                rhs_scale=ls[:],
+                start=True,
+                stop=True,
+            )
+            kbank[j, e] = kb
+
+        def k_out(j, e):
+            kt = work.tile([P, T], F32, name="kt%d" % e, bufs=2)
+            nc.scalar.activation(
+                out=kt[:], in_=kbank[j, e][:], func=ACT.Identity, bias=bqk[:, 1, j, e : e + 1], scale=1.0
+            )
+            kts[j, e] = kt
+
+        def q_mm(j, e):
+            wcode, wscal = wqw[j]
+            qb = psum.tile([P, T], F32, name="qb", tag="q", bufs=2)
+            for g in range(G):
+                c = slice(256 * g + P * e, 256 * g + P * (e + 1))
+                nc.tensor.matmul_mx(
+                    out=qb[:],
+                    lhsT=wcode[:, c].bitcast(FP8X4),
+                    lhsT_scale=wscal[:, c],
+                    rhs=xw[:, g, :].bitcast(FP8X4),
+                    rhs_scale=xs[:, g, :],
+                    start=(g == 0),
+                    stop=(g == G - 1),
+                )
+            qbank[j, e] = qb
+
+        def q_tab(j, e):
+            qt = work.tile([P, T], F32, name="qt%d" % e, bufs=2)
+            nc.vector.scalar_tensor_tensor(
+                out=b3(qt[:]), in0=b3(qbank[j, e][:]), scalar=bqk[:, 0, j, e : e + 1], in1=bc(tq[:, e, :]),
+                op0=ALU.add, op1=ALU.mult,
+            )
+            qts[j, e] = qt
+
+        def q_k(j, e):
+            pt = work.tile([P, T], F32, name="pt%d" % e, bufs=2)
+            nc.vector.scalar_tensor_tensor(
+                out=pt[:], in0=qbank[j, e][:], scalar=bqk[:, 0, j, e : e + 1], in1=kts[j, e][:],
+                op0=ALU.add, op1=ALU.mult,
+            )
+            pts[j, e] = pt
+
+        def eng_tt(eng, out_ap, a, b, op):
+            if eng == "v":
+                nc.vector.tensor_tensor(out=out_ap, in0=a, in1=b, op=op)
+            else:
+                nc.gpsimd.tensor_tensor(out=out_ap, in0=a, in1=b, op=op)
+
+        def k_tab(j, e, eng):
+            kc = work.tile([P, T], F32, name="kc%d" % e, bufs=2)
+            eng_tt(eng, b3(kc[:]), b3(kts[j, e][:]), bc(tk[:, e, :]), ALU.mult)
+            kcs[j, e] = kc
+
+        def k_rot(j, eng):
+            eng_tt(eng, kcs[j, 0][:], kcs[j, 0][:], kcs[j, 1][:], ALU.subtract)
+
+        def q_rot(j, eng):
+            eng_tt(eng, qts[j, 0][:], qts[j, 0][:], qts[j, 1][:], ALU.subtract)
+
+        def dot(j, eng):
+            eng_tt(eng, pts[j, 0][:], pts[j, 0][:], pts[j, 1][:], ALU.add)
+
+        def dot_rho(j, eng):
+            eng_tt(eng, b3(pts[j, 0][:]), b3(pts[j, 0][:]), bc(rho[:]), ALU.mult)
+
+        def z_even(j, eng):
+            ze = work.tile([P, T], F32, name="ze", bufs=2)
+            eng_tt(eng, ze[:], qts[j, 0][:], kcs[j, 0][:], ALU.mult)
+            zes[j] = ze
+
+        def z_odd(j, eng):
+            zo = work.tile([P, T], F32, name="zo", bufs=2)
+            eng_tt(eng, zo[:], pts[j, 0][:], zes[j][:], ALU.subtract)
+            zos[j] = zo
+
+        def z_tr(j, bb):
+            zb = psum.tile([P, 2, 2, P], F32, name="zb", tag="z", bufs=2)
+            for e, zz in ((0, zes[j]), (1, zos[j])):
+                for b in range(2):
+                    c = slice(P * (2 * bb + b), P * (2 * bb + b + 1))
+                    nc.tensor.transpose(zb[:, b, e, :], zz[:, c], ident[:])
+            zbank[j, bb] = zb
+
+        def z_min(j, bb):
+            nm = work.tile([P, 2, 2], F32, name="nm", bufs=4)
+            nc.vector.tensor_reduce(
+                out=nm[:],
+                in_=zbank[j, bb][:].rearrange("p b e (h i) -> p b h e i", h=2),
+                axis=AX.XY,
+                op=ALU.min,
+            )
+            nms[j, bb] = nm
+
+        def z_exp(j, bb):
+            et = work.tile([P, 2, 2, HD], F32, name="et", bufs=4)
+            sm = work.tile([P, 2, 2], F32, name="sm", bufs=4)
+            for b in range(2):
+                for h in range(2):
+                    nc.scalar.activation(
+                        out=et[:, b, h, :].rearrange("p (i e) -> p i e", e=2),
+                        in_=zbank[j, bb][:, b, :, PAIRS * h : PAIRS * (h + 1)].rearrange("p e i -> p i e"),
+                        func=ACT.Exp,
+                        bias=nms[j, bb][:, b, h : h + 1],
+                        scale=-1.0,
+                        accum_out=sm[:, b, h : h + 1],
+                    )
+            ets[j, bb] = et
+            sms[j, bb] = sm
+
+        def z_rcp(j, bb):
+            rs = work.tile([P, 2, 2], F32, name="rs", bufs=4)
+            nc.vector.reciprocal(out=rs[:], in_=sms[j, bb][:])
+            sms[j, bb] = rs
+
+        def z_norm(j, bb):
+            et = ets[j, bb]
+            for b in range(2):
+                for h in range(2):
+                    nc.scalar.activation(
+                        out=et[:, b, h, :], in_=et[:, b, h, :], func=ACT.Copy, scale=sms[j, bb][:, b, h : h + 1]
+                    )
+                nc.sync.dma_start(
+                    out=out[2 * bb + b, 2 * j : 2 * j + 2].rearrange("h s d -> s h d"), in_=et[:, b]
+                )
+
+
+        def widen2(j, half):
+            if j < J:
+                wq_widen(j, half, 0)
+                wq_widen(j, half, 1)
+
+        def tr(n):
+            if n < 4 * J:
+                wq_tr(n // 4, n % 4)
+
+        widen2(0, 0)
+        rows_tr("x", 0, 0)
+        rows_tr("x", 0, 1)
+        rows_out("x", 0, 0, "v")
+        rows_out("x", 0, 1, "v")
+        tr(0)
+        rows_tr("x", 1, 0)
+        rows_tr("x", 1, 1)
+        wq_scale(0, 0)
+        tr(1)
+        rows_out("x", 1, 0, "v")
+        rows_out("x", 1, 1, "s")
+        widen2(0, 1)
+        rows_tr("x", 2, 0)
+        rows_tr("x", 2, 1)
+        wq_scale(0, 1)
+        rows_out("x", 2, 0, "v")
+        rows_out("x", 2, 1, "s")
+        rows_tr("x", 3, 0)
+        rows_tr("x", 3, 1)
+        tr(2)
+        rows_out("x", 3, 0, "v")
+        rows_out("x", 3, 1, "s")
+        for g in range(G):
+            rows_quant("x", g, xw, xs)
+        rows_tr("d", 0, 0)
+        rows_tr("d", 0, 1)
+        wq_scale(0, 2)
+        tr(3)
+        rows_out("d", 0, 0, "s")
+        rows_out("d", 0, 1, "s")
+        rows_tr("d", 1, 0)
+        rows_tr("d", 1, 1)
+        wq_scale(0, 3)
+        rows_out("d", 1, 0, "s")
+        rows_out("d", 1, 1, "v")
+        rows_tr("d", 2, 0)
+        rows_tr("d", 2, 1)
+        wq_quant(0)
+        rows_out("d", 2, 0, "s")
+        rows_out("d", 2, 1, "v")
+        rows_tr("d", 3, 0)
+        rows_tr("d", 3, 1)
+        rows_out("d", 3, 0, "s")
+        rows_out("d", 3, 1, "v")
+        widen2(1, 0)
+        biases()
+        wuk_tr(0)
+        wuk_out(0, "s")
+        for g in range(G):
+            rows_quant("d", g, dw, ds)
+        tr(4)
+        lkv_mm(0)
+        wq_scale(1, 0)
+        widen2(1, 1)
+        lkv_mm(1)
+        lkv_out(0)
+        tr(5)
+        wuk_quant(0)
+        wuk_tr(1)
+        wuk_out(1, "s")
+        lkv_mm(2)
+        lkv_out(1)
+        wq_scale(1, 1)
+        tr(6)
+        lkv_mm(3)
+        lkv_out(2)
+        lkv_out(3)
+        wuk_quant(1)
+        lkv_quant()
+        q_mm(0, 0)
+        k_mm(0, 0)
+        k_out(0, 0)
+        k_mm(0, 1)
+        k_out(0, 1)
+        q_mm(0, 1)
+
+        def step(j):
+            a = j + 1
+            has_a = a < J
+            p = j - 1
+            has_p = p >= 0
+            ge = "g" if has_a else "v"
+            k_tab(j, 0, "g")
+            k_tab(j, 1, "g")
+            k_rot(j, "g")
+            widen2(j + 2, 0)
+            if has_a and j > 0:
+                wq_scale(a, 0)
+                tr(4 * a + 2)
+            q_tab(j, 0)
+            q_k(j, 0)
+            q_tab(j, 1)
+            q_k(j, 1)
+            q_rot(j, ge)
+            z_even(j, ge)
+            dot(j, ge)
+            dot_rho(j, ge)
+            if has_a:
+                if j > 0:
+                    wq_scale(a, 1)
+                tr(4 * a + 3)
+            if has_p:
+                z_min(p, 0)
+                z_min(p, 1)
+                z_exp(p, 0)
+                z_exp(p, 1)
+            if has_a:
+                k_mm(a, 0)
+            if a + 1 < J:
+                wuk_tr(a + 1)
+                wuk_out(a + 1, "s")
+            widen2(j + 2, 1)
+            if has_a:
+                wq_scale(a, 2)
+                tr(4 * a + 4)
+                wq_scale(a, 3)
+                tr(4 * a + 5)
+            if has_p:
+                for bb in range(2):
+                    z_rcp(p, bb)
+                    z_norm(p, bb)
+            if has_a:
+                wq_quant(a)
+                q_mm(a, 0)
+                k_out(a, 0)
+                k_mm(a, 1)
+                k_out(a, 1)
+                q_mm(a, 1)
+            if a + 1 < J:
+                wuk_quant(a + 1)
+            z_odd(j, "v")
+            z_tr(j, 0)
+            z_tr(j, 1)
+
+        for j in range(J):
+            step(j)
+        for bb in range(2):
+            z_min(J - 1, bb)
+            z_exp(J - 1, bb)
+        for bb in range(2):
+            z_rcp(J - 1, bb)
+            z_norm(J - 1, bb)

@@ -20,7 +20,7 @@ T = B * S
 P = 128
 G = DIM // 512
 J = H // 2
-KAPPA = DIM ** -0.5
+KAPPA = DIM**-0.5
 
 FLOPS = 2 * T * (DIM * KV + DIM * DIM + KV * DIM)
 
@@ -34,30 +34,39 @@ def tile_multilatentattention_pa_kernel(
         keep = ctx.enter_context(tc.tile_pool(name="keep", bufs=1))
         work = ctx.enter_context(tc.tile_pool(name="work", bufs=2))
         psum = ctx.enter_context(tc.psum_pool(name="psum", bufs=1))
+        BANKS = {"w": 3, "q": 2, "z": 2, "k": 1}
 
         ident = keep.tile([P, P], F32, name="ident")
         make_identity(nc, ident[:])
         warm = keep.tile([P, 1], F32, name="warm")
         nc.vector.memset(warm[:], 0.0)
         nc.scalar.activation(out=warm[:], in_=warm[:], func=ACT.Exp)
-        cs_raw = keep.tile([P, 2, 2, PAIRS], BF16, name="cs_raw")
-        sc = keep.tile([P, G * 4], F32, name="sc")
-        for h in range(2):
-            nc.sync.dma_start(out=cs_raw[:, 0, h, :], in_=rope_cos)
-            nc.sync.dma_start(out=cs_raw[:, 1, h, :], in_=rope_sin)
+
+        wq_sc = keep.tile([P, G * 4], F32, name="wq_sc")
         nc.sync.dma_start(
-            out=sc[:].rearrange("p (g t) -> p g t", t=4),
+            out=wq_sc[:].rearrange("p (g t) -> p g t", t=4),
             in_=Wq_scale.rearrange("o (g p t) -> p (o g) t", p=P, t=4),
         )
+        bd_raw = keep.tile([P, 4], BF16, name="bd_raw")
+        nc.gpsimd.dma_start(out=bd_raw[:], in_=b_kv_down.rearrange("(p t) -> p t", t=4))
+        bqk_raw = keep.tile([P, 2, J, 2], BF16, name="bqk_raw")
+        nc.gpsimd.dma_start(out=bqk_raw[:, 0], in_=bq.rearrange("(j p e) -> p j e", p=P, e=2))
+        nc.gpsimd.dma_start(out=bqk_raw[:, 1], in_=b_uk.rearrange("(j p e) -> p j e", p=P, e=2))
+        cs_raw = keep.tile([P, 2, 2, PAIRS], BF16, name="cs_raw")
         raws = {}
-        byts = {}
+        wq_bytes = {}
+
+        def load_rope():
+            for h in range(2):
+                nc.sync.dma_start(out=cs_raw[:, 0, h, :], in_=rope_cos)
+                nc.sync.dma_start(out=cs_raw[:, 1, h, :], in_=rope_sin)
 
         def load_x(b):
             raw = work.tile([P, DIM], BF16, name="raw", bufs=8)
             nc.sync.dma_start(out=raw[:], in_=x[b])
             raws["x", b] = raw
 
-        def load_wd(t):
+        def load_wdown(t):
             raw = work.tile([P, DIM], BF16, name="raw", bufs=8)
             nc.sync.dma_start(out=raw[:], in_=W_kv_down.rearrange("(m t) k -> t m k", t=4)[t])
             raws["d", t] = raw
@@ -70,79 +79,54 @@ def tile_multilatentattention_pa_kernel(
             )
             raws["u", jj] = raw
 
-        def load_wq(j, halves=1):
-            byt = keep.tile([P, 2, DIM], U8, name="wq_bytes_%d" % j)
-            byts[j] = byt
-            return byt
-
-        def load_wq_part(j, c):
+        def load_wq(j, k0=0, k1=DIM):
+            if j not in wq_bytes:
+                byt = work.tile([P, 2, DIM], U8, name="byt", bufs=4)
+                wq_bytes[j] = byt
             nc.sync.dma_start(
-                out=byts[j][:, :, c],
-                in_=Wq_bytes.rearrange("(j p e) k -> j p e k", p=P, e=2)[j][:, :, c],
+                out=wq_bytes[j][:, :, k0:k1],
+                in_=Wq_bytes.rearrange("(j p e) k -> j p e k", p=P, e=2)[j][:, :, k0:k1],
             )
 
-        full = slice(0, DIM)
-        for j in range(J):
-            load_wq(j)
-        load_wq_part(0, slice(0, DIM // 2))
-        load_x(0)
-        load_wq_part(0, slice(DIM // 2, DIM))
-        load_x(1)
-        load_x(2)
-        load_x(3)
-        load_wq_part(1, full)
-        load_wd(0)
-        load_wd(1)
-        load_wd(2)
-        load_wd(3)
-        load_wq_part(2, full)
-        load_wuk(0)
-        load_wq_part(3, full)
-        load_wuk(1)
-        load_wq_part(4, full)
-        load_wq_part(5, full)
-        load_wuk(2)
-        load_wq_part(6, full)
-        load_wq_part(7, full)
-        load_wuk(3)
-
-        bd_raw = keep.tile([P, 4], BF16, name="bd_raw")
-        nc.gpsimd.dma_start(out=bd_raw[:], in_=b_kv_down.rearrange("(p t) -> p t", t=4))
-        bqk_raw = keep.tile([P, 2, J, 2], BF16, name="bqk_raw")
-        nc.gpsimd.dma_start(out=bqk_raw[:, 0], in_=bq.rearrange("(j p e) -> p j e", p=P, e=2))
-        nc.gpsimd.dma_start(out=bqk_raw[:, 1], in_=b_uk.rearrange("(j p e) -> p j e", p=P, e=2))
-
         csf = keep.tile([P, 2, P], F32, name="csf")
-        nc.vector.tensor_copy(out=csf[:], in_=cs_raw[:].rearrange("p a h i -> p a (h i)"))
-        tabs_ps = psum.tile([P, 2, P], F32, name="tabs_ps", tag="z", bufs=2)
-        for a in range(2):
-            nc.tensor.transpose(tabs_ps[:, a, :], csf[:, a, :], ident[:])
         tk = keep.tile([P, 2, P], F32, name="tk")
-        nc.vector.tensor_copy(out=tk[:], in_=tabs_ps[:])
         tq = keep.tile([P, 2, P], F32, name="tq")
-        nc.vector.tensor_scalar(out=tq[:], in0=tk[:], scalar1=-KAPPA, scalar2=None, op0=ALU.mult)
         rr = keep.tile([P, 2, P], F32, name="rr")
-        nc.vector.tensor_tensor(out=rr[:], in0=tk[:], in1=tq[:], op=ALU.mult)
         rho = keep.tile([P, P], F32, name="rho")
-        nc.vector.tensor_tensor(out=rho[:], in0=rr[:, 0, :], in1=rr[:, 1, :], op=ALU.add)
         bd = keep.tile([P, 4], F32, name="bd")
         bqk = keep.tile([P, 2, J, 2], F32, name="bqk")
+        tbank = {}
+
+        def rope_widen():
+            nc.scalar.copy(csf[:], cs_raw[:].rearrange("p a h i -> p a (h i)"))
+
+        def rope_transpose():
+            bank = psum.tile([P, 2, P], F32, name="rope_bank", tag="z", bufs=BANKS["z"])
+            for a in range(2):
+                nc.tensor.transpose(bank[:, a, :], csf[:, a, :], ident[:])
+            tbank[0] = bank
+
+        def rope_key():
+            nc.scalar.copy(tk[:], tbank[0][:])
+
+        def rope_query():
+            nc.scalar.activation(out=tq[:], in_=tk[:], func=ACT.Copy, scale=-KAPPA)
+
+        def rope_squares():
+            nc.gpsimd.tensor_tensor(out=rr[:], in0=tk[:], in1=tq[:], op=ALU.mult)
+
+        def rope_rho():
+            nc.gpsimd.tensor_tensor(out=rho[:], in0=rr[:, 0, :], in1=rr[:, 1, :], op=ALU.add)
 
         def biases():
-            nc.vector.tensor_copy(out=bd[:], in_=bd_raw[:])
-            nc.vector.tensor_copy(out=bqk[:], in_=bqk_raw[:])
+            nc.scalar.copy(bd[:], bd_raw[:])
+            nc.scalar.copy(bqk[:], bqk_raw[:])
 
-        def bc(tab):
+        def over_batches(tab):
             return tab.unsqueeze(1).to_broadcast([P, B, S])
 
-        def b3(ap):
+        def by_batch(ap):
             return ap.rearrange("p (b s) -> p b s", b=B)
-
-        xw = keep.tile([P, G, T], U32, name="xw", align_bytes=64)
-        xs = keep.tile([P, G, T], U8, name="xs", align_bytes=64)
-        dw = keep.tile([P, G, KV], U32, name="dw", align_bytes=64)
-        ds = keep.tile([P, G, KV], U8, name="ds", align_bytes=64)
-        grps = {}
 
         def copy_out(eng, out_ap, in_ap):
             if eng == "v":
@@ -150,124 +134,142 @@ def tile_multilatentattention_pa_kernel(
             else:
                 nc.scalar.copy(out_ap, in_ap)
 
-        rbank = {}
+        def elementwise(eng, out_ap, a, b, op):
+            if eng == "v":
+                nc.vector.tensor_tensor(out=out_ap, in0=a, in1=b, op=op)
+            else:
+                nc.gpsimd.tensor_tensor(out=out_ap, in0=a, in1=b, op=op)
 
-        def rows_tr(kind, b, gg):
+        def keep_busy(bank_ap, n):
+            for i in range(n):
+                nc.tensor.matmul(bank_ap, lhsT=ident[:], rhs=ident[:], start=True, stop=True)
+
+        xw = keep.tile([P, G, T], U32, name="xw", align_bytes=64)
+        xs = keep.tile([P, G, T], U8, name="xs", align_bytes=64)
+        dw = keep.tile([P, G, KV], U32, name="dw", align_bytes=64)
+        ds = keep.tile([P, G, KV], U8, name="ds", align_bytes=64)
+        codes = {"x": (xw, xs), "d": (dw, ds)}
+        row_banks = {}
+        groups = {}
+
+        def rows_transpose(kind, b, gg, busy, tag):
             words = raws[kind, b][:].bitcast(F32)
-            bank = psum.tile([P, 2, 2, P], F32, name="bank", tag="w", bufs=3)
+            bank = psum.tile([P, 2, 2, P], F32, name="row_bank", tag=tag, bufs=BANKS[tag])
+            keep_busy(bank[:, 0, 0, :], busy)
             for g2 in range(2):
                 g = 2 * gg + g2
                 for u in range(2):
-                    nc.tensor.transpose(
-                        bank[:, g2, u, :], words[:, 256 * g + u : 256 * (g + 1) : 2], ident[:]
-                    )
-            rbank[kind, b, gg] = bank
+                    nc.tensor.transpose(bank[:, g2, u, :], words[:, 256 * g + u : 256 * (g + 1) : 2], ident[:])
+            row_banks[kind, b, gg] = bank
 
         def rows_out(kind, b, gg, eng):
-            if kind not in grps:
-                grp = work.tile([P, G, T, 4], BF16, name="grp2048", bufs=1, align_bytes=64)
-                grps[kind] = grp
-            dst = grps[kind][:, 2 * gg : 2 * gg + 2, P * b : P * (b + 1), :]
+            if (kind, gg) not in groups:
+                grp = work.tile([P, 2, T, 4], BF16, name="grp", bufs=3, align_bytes=64)
+                groups[kind, gg] = grp
+            dst = groups[kind, gg][:, :, P * b : P * (b + 1), :]
             copy_out(
                 eng,
                 dst.rearrange("p g n t -> p g (n t)").bitcast(F32).rearrange("p g (n u) -> p g n u", u=2),
-                rbank[kind, b, gg][:].rearrange("p g u n -> p g n u"),
+                row_banks[kind, b, gg][:].rearrange("p g u n -> p g n u"),
             )
 
-        def rows_quant(kind, g, words, scales):
+        def rows_quantise(kind, g):
+            words, scales = codes[kind]
             nc.vector.quantize_mx(
                 out=words[:, g, :].bitcast(FP8X4),
                 scales=scales[:, g, :],
-                in_=grps[kind][:, g].rearrange("p n t -> p (n t)"),
+                in_=groups[kind, g // 2][:, g % 2].rearrange("p n t -> p (n t)"),
             )
 
         wides = {}
-        wqg = {}
-        wqw = {}
+        wq_banks = {}
+        wq_groups = {}
+        wq_codes = {}
 
-        def wq_widen(j, half, e):
+        def wide_tile(j):
             if j not in wides:
-                wide = work.tile([P, 2, DIM], BF16, name="wide", bufs=2)
+                wide = work.tile([P, 2, DIM], BF16, name="wide", bufs=3)
                 wides[j] = wide
-            c = slice(1024 * half, 1024 * (half + 1))
-            nc.scalar.copy(wides[j][:, e, c], byts[j][:, e, c].bitcast(FP8))
+            return wides[j]
 
-        wbank = {}
+        def wq_widen(j, e, k0=0, k1=DIM):
+            if j < J:
+                nc.scalar.copy(wide_tile(j)[:, e, k0:k1], wq_bytes[j][:, e, k0:k1].bitcast(FP8))
 
-        def wq_tr(j, g):
-            bank = psum.tile([P, 2, 256], F32, name="wbank", tag="w", bufs=3)
-            for e in range(2):
-                words = wides[j][:, e, :].bitcast(F32)
-                for u in range(2):
-                    nc.tensor.transpose(
-                        bank[:, u, P * e : P * (e + 1)],
-                        words[:, 256 * g + u : 256 * (g + 1) : 2],
-                        ident[:],
-                    )
-            wbank[j, g] = bank
+        def wq_transpose(j, g, busy=0):
+            if j < J:
+                bank = psum.tile([P, 2, 256], F32, name="wq_bank", tag="w", bufs=BANKS["w"])
+                keep_busy(bank[:, 0, 0:P], busy)
+                for e in range(2):
+                    words = wides[j][:, e, :].bitcast(F32)
+                    for u in range(2):
+                        nc.tensor.transpose(
+                            bank[:, u, P * e : P * (e + 1)],
+                            words[:, 256 * g + u : 256 * (g + 1) : 2],
+                            ident[:],
+                        )
+                wq_banks[j, g] = bank
 
-        def wq_scale(j, g):
-            if j not in wqg:
-                grp = work.tile([P, G, 256 * 4], BF16, name="wqgrp", bufs=2, align_bytes=64)
-                wqg[j] = grp
+        def wq_scale_out(j, g):
+            if j not in wq_groups:
+                wgrp = work.tile([P, G, 256 * 4], BF16, name="wgrp", bufs=2, align_bytes=64)
+                wq_groups[j] = wgrp
             nc.vector.tensor_tensor(
-                out=wqg[j][:, g, :].rearrange("p (n u e) -> p n u e", u=2, e=2),
-                in0=wbank[j, g][:].bitcast(BF16).rearrange("p u (n e) -> p n u e", e=2),
-                in1=sc[:, 4 * g : 4 * g + 4]
+                out=wq_groups[j][:, g, :].rearrange("p (n u e) -> p n u e", u=2, e=2),
+                in0=wq_banks[j, g][:].bitcast(BF16).rearrange("p u (n e) -> p n u e", e=2),
+                in1=wq_sc[:, 4 * g : 4 * g + 4]
                 .rearrange("p (u e) -> p u e", e=2)
                 .unsqueeze(1)
                 .to_broadcast([P, 256, 2, 2]),
                 op=ALU.mult,
             )
 
-        def wq_quant(j):
-            wcode = work.tile([P, G * 256], U32, name="wqcode", bufs=3, align_bytes=64)
-            wscal = work.tile([P, G * 256], U8, name="wqscal", bufs=3, align_bytes=64)
+        def wq_quantise(j):
+            wcode = work.tile([P, G * 256], U32, name="wcode", bufs=3, align_bytes=64)
+            wscal = work.tile([P, G * 256], U8, name="wscal", bufs=3, align_bytes=64)
             nc.vector.quantize_mx(
                 out=wcode[:].bitcast(FP8X4),
                 scales=wscal[:],
-                in_=wqg[j][:].rearrange("p g c -> p (g c)"),
+                in_=wq_groups[j][:].rearrange("p g c -> p (g c)"),
             )
-            wqw[j] = (wcode, wscal)
+            wq_codes[j] = (wcode, wscal)
 
         uw = keep.tile([P, J, 2, P], U32, name="uw", align_bytes=64)
         us = keep.tile([P, J, 2, P], U8, name="us", align_bytes=64)
+        wuk_banks = {}
+        wuk_groups = {}
 
-        ubank = {}
-        ugs = {}
-
-        def wuk_tr(j):
-            bank = psum.tile([P, 2, 2, P], F32, name="ubank", tag="w", bufs=3)
+        def wuk_transpose(j):
+            bank = psum.tile([P, 2, 2, P], F32, name="wuk_bank", tag="w", bufs=BANKS["w"])
             words = raws["u", j // 2][:].bitcast(F32).rearrange("p (j e w) -> p j e w", j=2, e=2)
             for e in range(2):
                 for u in range(2):
                     nc.tensor.transpose(bank[:, e, u, :], words[:, j % 2, e, u:256:2], ident[:])
-            ubank[j] = bank
+            wuk_banks[j] = bank
 
         def wuk_out(j, eng):
-            ug = work.tile([P, 2, P, 4], BF16, name="ug", bufs=2, align_bytes=64)
+            ugrp = work.tile([P, 2, P, 4], BF16, name="ugrp", bufs=2, align_bytes=64)
             copy_out(
                 eng,
-                ug[:].rearrange("p e n t -> p e (n t)").bitcast(F32).rearrange("p e (n u) -> p e n u", u=2),
-                ubank[j][:].rearrange("p e u n -> p e n u"),
+                ugrp[:].rearrange("p e n t -> p e (n t)").bitcast(F32).rearrange("p e (n u) -> p e n u", u=2),
+                wuk_banks[j][:].rearrange("p e u n -> p e n u"),
             )
-            ugs[j] = ug
+            wuk_groups[j] = ugrp
 
-        def wuk_quant(j):
+        def wuk_quantise(j):
             nc.vector.quantize_mx(
                 out=uw[:, j].rearrange("p e n -> p (e n)").bitcast(FP8X4),
                 scales=us[:, j].rearrange("p e n -> p (e n)"),
-                in_=ugs[j][:].rearrange("p e n t -> p (e n t)"),
+                in_=wuk_groups[j][:].rearrange("p e n t -> p (e n t)"),
             )
 
         lg = keep.tile([P, T, 4], BF16, name="lg", align_bytes=64)
         lw = keep.tile([P, T], U32, name="lw", align_bytes=64)
         ls = keep.tile([P, T], U8, name="ls", align_bytes=64)
+        lkv_banks = {}
 
-        lbank = {}
-
-        def lkv_mm(b):
-            bank = psum.tile([P, 4, P], F32, name="lbank", tag="q", bufs=2)
+        def lkv_matmul(b):
+            bank = psum.tile([P, 4, P], F32, name="lkv_bank", tag="z", bufs=BANKS["z"])
             for t in range(4):
                 for g in range(G):
                     nc.tensor.matmul_mx(
@@ -279,38 +281,35 @@ def tile_multilatentattention_pa_kernel(
                         start=(g == 0),
                         stop=(g == G - 1),
                     )
-            lbank[b] = bank
+            lkv_banks[b] = bank
 
         def lkv_out(b):
             nc.vector.tensor_tensor(
                 out=lg[:, P * b : P * (b + 1), :],
-                in0=lbank[b][:].rearrange("p t n -> p n t"),
+                in0=lkv_banks[b][:].rearrange("p t n -> p n t"),
                 in1=bd[:].unsqueeze(1).to_broadcast([P, P, 4]),
                 op=ALU.add,
             )
 
-        def lkv_quant():
+        def lkv_quantise():
             nc.vector.quantize_mx(
                 out=lw[:].bitcast(FP8X4), scales=ls[:], in_=lg[:].rearrange("p n t -> p (n t)")
             )
 
-        kbank = {}
+        k_banks = {}
+        q_banks = {}
         kts = {}
-        qbank = {}
+        kcs = {}
         qts = {}
         pts = {}
-        kcs = {}
+        dot_banks = {}
         zes = {}
         zos = {}
-        zbank = {}
-        nms = {}
-        sms = {}
-        ets = {}
 
-        def k_mm(j, e):
-            kb = psum.tile([P, T], F32, name="kb", tag="k", bufs=1)
+        def k_matmul(j, e):
+            bank = psum.tile([P, T], F32, name="k_bank", tag="k", bufs=BANKS["k"])
             nc.tensor.matmul_mx(
-                out=kb[:],
+                out=bank[:],
                 lhsT=uw[:, j, e, :].bitcast(FP8X4),
                 lhsT_scale=us[:, j, e, :],
                 rhs=lw[:].bitcast(FP8X4),
@@ -318,22 +317,22 @@ def tile_multilatentattention_pa_kernel(
                 start=True,
                 stop=True,
             )
-            kbank[j, e] = kb
+            k_banks[j, e] = bank
 
-        def k_out(j, e):
+        def k_bias(j, e):
             kt = work.tile([P, T], F32, name="kt%d" % e, bufs=2)
             nc.scalar.activation(
-                out=kt[:], in_=kbank[j, e][:], func=ACT.Identity, bias=bqk[:, 1, j, e : e + 1], scale=1.0
+                out=kt[:], in_=k_banks[j, e][:], func=ACT.Identity, bias=bqk[:, 1, j, e : e + 1], scale=1.0
             )
             kts[j, e] = kt
 
-        def q_mm(j, e):
-            wcode, wscal = wqw[j]
-            qb = psum.tile([P, T], F32, name="qb", tag="q", bufs=2)
+        def q_matmul(j, e):
+            wcode, wscal = wq_codes[j]
+            bank = psum.tile([P, T], F32, name="q_bank", tag="q", bufs=BANKS["q"])
             for g in range(G):
                 c = slice(256 * g + P * e, 256 * g + P * (e + 1))
                 nc.tensor.matmul_mx(
-                    out=qb[:],
+                    out=bank[:],
                     lhsT=wcode[:, c].bitcast(FP8X4),
                     lhsT_scale=wscal[:, c],
                     rhs=xw[:, g, :].bitcast(FP8X4),
@@ -341,257 +340,354 @@ def tile_multilatentattention_pa_kernel(
                     start=(g == 0),
                     stop=(g == G - 1),
                 )
-            qbank[j, e] = qb
+            q_banks[j, e] = bank
 
-        def q_tab(j, e):
+        def q_table(j, e):
             qt = work.tile([P, T], F32, name="qt%d" % e, bufs=2)
             nc.vector.scalar_tensor_tensor(
-                out=b3(qt[:]), in0=b3(qbank[j, e][:]), scalar=bqk[:, 0, j, e : e + 1], in1=bc(tq[:, e, :]),
-                op0=ALU.add, op1=ALU.mult,
+                out=by_batch(qt[:]), in0=by_batch(q_banks[j, e][:]), scalar=bqk[:, 0, j, e : e + 1],
+                in1=over_batches(tq[:, e, :]), op0=ALU.add, op1=ALU.mult,
             )
             qts[j, e] = qt
 
-        def q_k(j, e):
+        def q_times_k(j, e):
             pt = work.tile([P, T], F32, name="pt%d" % e, bufs=2)
             nc.vector.scalar_tensor_tensor(
-                out=pt[:], in0=qbank[j, e][:], scalar=bqk[:, 0, j, e : e + 1], in1=kts[j, e][:],
+                out=pt[:], in0=q_banks[j, e][:], scalar=bqk[:, 0, j, e : e + 1], in1=kts[j, e][:],
                 op0=ALU.add, op1=ALU.mult,
             )
             pts[j, e] = pt
 
-        def eng_tt(eng, out_ap, a, b, op):
-            if eng == "v":
-                nc.vector.tensor_tensor(out=out_ap, in0=a, in1=b, op=op)
-            else:
-                nc.gpsimd.tensor_tensor(out=out_ap, in0=a, in1=b, op=op)
-
-        def k_tab(j, e, eng):
+        def k_table(j, e):
             kc = work.tile([P, T], F32, name="kc%d" % e, bufs=2)
-            eng_tt(eng, b3(kc[:]), b3(kts[j, e][:]), bc(tk[:, e, :]), ALU.mult)
+            elementwise("g", by_batch(kc[:]), by_batch(kts[j, e][:]), over_batches(tk[:, e, :]), ALU.mult)
             kcs[j, e] = kc
 
-        def k_rot(j, eng):
-            eng_tt(eng, kcs[j, 0][:], kcs[j, 0][:], kcs[j, 1][:], ALU.subtract)
+        def k_rotate(j, eng):
+            elementwise(eng, kcs[j, 0][:], kcs[j, 0][:], kcs[j, 1][:], ALU.subtract)
 
-        def q_rot(j, eng):
-            eng_tt(eng, qts[j, 0][:], qts[j, 0][:], qts[j, 1][:], ALU.subtract)
+        def q_rotate(j, eng):
+            elementwise(eng, qts[j, 0][:], qts[j, 0][:], qts[j, 1][:], ALU.subtract)
 
-        def dot(j, eng):
-            eng_tt(eng, pts[j, 0][:], pts[j, 0][:], pts[j, 1][:], ALU.add)
+        def dot(j):
+            bank = psum.tile([P, T], F32, name="dot_bank", tag="k", bufs=BANKS["k"])
+            for e in range(2):
+                nc.tensor.matmul(bank[:], lhsT=ident[:], rhs=pts[j, e][:], start=(e == 0), stop=(e == 1))
+            dot_banks[j] = bank
 
-        def dot_rho(j, eng):
-            eng_tt(eng, b3(pts[j, 0][:]), b3(pts[j, 0][:]), bc(rho[:]), ALU.mult)
+        def dot_rho(j):
+            nc.vector.tensor_tensor(
+                out=by_batch(pts[j, 0][:]), in0=by_batch(dot_banks[j][:]), in1=over_batches(rho[:]), op=ALU.mult
+            )
 
         def z_even(j, eng):
             ze = work.tile([P, T], F32, name="ze", bufs=2)
-            eng_tt(eng, ze[:], qts[j, 0][:], kcs[j, 0][:], ALU.mult)
+            elementwise(eng, ze[:], qts[j, 0][:], kcs[j, 0][:], ALU.mult)
             zes[j] = ze
 
         def z_odd(j, eng):
             zo = work.tile([P, T], F32, name="zo", bufs=2)
-            eng_tt(eng, zo[:], pts[j, 0][:], zes[j][:], ALU.subtract)
+            elementwise(eng, zo[:], pts[j, 0][:], zes[j][:], ALU.subtract)
             zos[j] = zo
 
-        def z_tr(j, bb):
-            zb = psum.tile([P, 2, 2, P], F32, name="zb", tag="z", bufs=2)
+        def last_z(j, bb):
+            c = slice(2 * S * bb, 2 * S * (bb + 1))
+            if bb == 0:
+                ze = work.tile([P, T], F32, name="ze", bufs=2)
+                zo = work.tile([P, T], F32, name="zo", bufs=2)
+                zes[j] = ze
+                zos[j] = zo
+            ze = zes[j]
+            zo = zos[j]
+            qc = qts[j, 0][:, c]
+            pa = pts[j, 0][:, c]
+            pa2 = pa.rearrange("p (b s) -> p b s", b=2)
+            nc.vector.tensor_tensor(out=qc, in0=qc, in1=qts[j, 1][:, c], op=ALU.subtract)
+            nc.vector.tensor_tensor(out=pa, in0=pa, in1=pts[j, 1][:, c], op=ALU.add)
+            nc.vector.tensor_tensor(out=ze[:, c], in0=qc, in1=kcs[j, 0][:, c], op=ALU.mult)
+            nc.vector.tensor_tensor(
+                out=pa2, in0=pa2, in1=rho[:].unsqueeze(1).to_broadcast([P, 2, S]), op=ALU.mult
+            )
+            nc.vector.tensor_tensor(out=zo[:, c], in0=pa, in1=ze[:, c], op=ALU.subtract)
+
+        z_banks = {}
+        minima = {}
+        sums = {}
+        reciprocals = {}
+        exps = {}
+
+        def z_transpose(j, bb):
+            tag = "w" if j == J - 1 else "z"
+            bank = psum.tile([P, 2, 2, P], F32, name="z_bank", tag=tag, bufs=BANKS[tag])
             for e, zz in ((0, zes[j]), (1, zos[j])):
                 for b in range(2):
                     c = slice(P * (2 * bb + b), P * (2 * bb + b + 1))
-                    nc.tensor.transpose(zb[:, b, e, :], zz[:, c], ident[:])
-            zbank[j, bb] = zb
+                    nc.tensor.transpose(bank[:, b, e, :], zz[:, c], ident[:])
+            z_banks[j, bb] = bank
 
         def z_min(j, bb):
             nm = work.tile([P, 2, 2], F32, name="nm", bufs=4)
             nc.vector.tensor_reduce(
                 out=nm[:],
-                in_=zbank[j, bb][:].rearrange("p b e (h i) -> p b h e i", h=2),
+                in_=z_banks[j, bb][:].rearrange("p b e (h i) -> p b h e i", h=2),
                 axis=AX.XY,
                 op=ALU.min,
             )
-            nms[j, bb] = nm
+            minima[j, bb] = nm
 
         def z_exp(j, bb):
             et = work.tile([P, 2, 2, HD], F32, name="et", bufs=4)
-            sm = work.tile([P, 2, 2], F32, name="sm", bufs=4)
+            if j not in sums:
+                sm = work.tile([P, 2, 2, 2], F32, name="sm", bufs=2)
+                sums[j] = sm
             for b in range(2):
                 for h in range(2):
                     nc.scalar.activation(
                         out=et[:, b, h, :].rearrange("p (i e) -> p i e", e=2),
-                        in_=zbank[j, bb][:, b, :, PAIRS * h : PAIRS * (h + 1)].rearrange("p e i -> p i e"),
+                        in_=z_banks[j, bb][:, b, :, PAIRS * h : PAIRS * (h + 1)].rearrange("p e i -> p i e"),
                         func=ACT.Exp,
-                        bias=nms[j, bb][:, b, h : h + 1],
+                        bias=minima[j, bb][:, b, h : h + 1],
                         scale=-1.0,
-                        accum_out=sm[:, b, h : h + 1],
+                        accum_out=sums[j][:, bb, b, h : h + 1],
                     )
-            ets[j, bb] = et
-            sms[j, bb] = sm
+            exps[j, bb] = et
 
-        def z_rcp(j, bb):
-            rs = work.tile([P, 2, 2], F32, name="rs", bufs=4)
-            nc.vector.reciprocal(out=rs[:], in_=sms[j, bb][:])
-            sms[j, bb] = rs
+        def z_reciprocal(j, b0, b1):
+            if j not in reciprocals:
+                rs = work.tile([P, 2, 2, 2], F32, name="rs", bufs=2)
+                reciprocals[j] = rs
+            nc.vector.reciprocal(out=reciprocals[j][:, b0:b1], in_=sums[j][:, b0:b1])
 
-        def z_norm(j, bb):
-            et = ets[j, bb]
+        def z_store(j, bb, eng):
+            et = exps[j, bb]
             for b in range(2):
                 for h in range(2):
-                    nc.scalar.activation(
-                        out=et[:, b, h, :], in_=et[:, b, h, :], func=ACT.Copy, scale=sms[j, bb][:, b, h : h + 1]
-                    )
+                    r = reciprocals[j][:, bb, b, h : h + 1]
+                    if eng == "v":
+                        nc.vector.tensor_scalar(
+                            out=et[:, b, h, :], in0=et[:, b, h, :], scalar1=r, scalar2=None, op0=ALU.mult
+                        )
+                    else:
+                        nc.scalar.activation(out=et[:, b, h, :], in_=et[:, b, h, :], func=ACT.Copy, scale=r)
+            for b in range(2):
                 nc.sync.dma_start(
                     out=out[2 * bb + b, 2 * j : 2 * j + 2].rearrange("h s d -> s h d"), in_=et[:, b]
                 )
 
-
-        def widen2(j, half):
-            if j < J:
-                wq_widen(j, half, 0)
-                wq_widen(j, half, 1)
-
-        def tr(n):
-            if n < 4 * J:
-                wq_tr(n // 4, n % 4)
-
-        widen2(0, 0)
-        rows_tr("x", 0, 0)
-        rows_tr("x", 0, 1)
-        rows_out("x", 0, 0, "v")
-        rows_out("x", 0, 1, "v")
-        tr(0)
-        rows_tr("x", 1, 0)
-        rows_tr("x", 1, 1)
-        wq_scale(0, 0)
-        tr(1)
+        load_x(3)
+        load_x(1)
+        load_wq(0, 1024, 2048)
+        rows_transpose("x", 3, 0, 3, "w")
+        wq_widen(0, 0, 1024, 2048)
+        rows_transpose("x", 1, 0, 2, "q")
+        load_x(0)
+        load_wdown(3)
+        wq_widen(0, 1, 1024, 2048)
         rows_out("x", 1, 0, "v")
+        load_wq(0, 0, 1024)
+        wq_widen(0, 0, 0, 1024)
+        rows_transpose("x", 3, 1, 0, "q")
+        load_wuk(0)
+        rows_transpose("x", 1, 1, 2, "w")
+        rows_out("x", 3, 1, "v")
+        rows_transpose("x", 0, 1, 0, "q")
         rows_out("x", 1, 1, "s")
-        widen2(0, 1)
-        rows_tr("x", 2, 0)
-        rows_tr("x", 2, 1)
-        wq_scale(0, 1)
-        rows_out("x", 2, 0, "v")
-        rows_out("x", 2, 1, "s")
-        rows_tr("x", 3, 0)
-        rows_tr("x", 3, 1)
-        tr(2)
+        wq_transpose(0, 2, busy=2)
         rows_out("x", 3, 0, "v")
-        rows_out("x", 3, 1, "s")
-        for g in range(G):
-            rows_quant("x", g, xw, xs)
-        rows_tr("d", 0, 0)
-        rows_tr("d", 0, 1)
-        wq_scale(0, 2)
-        tr(3)
+        load_x(2)
+        wq_transpose(0, 3)
+        rows_out("x", 0, 1, "v")
+        wq_widen(0, 1, 0, 1024)
+        rows_transpose("x", 0, 0, 0, "q")
+        wq_transpose(0, 0, busy=2)
+        rows_transpose("x", 2, 0, 0, "z")
+        rows_transpose("x", 2, 1, 2, "q")
+        rows_out("x", 2, 0, "s")
+        wq_scale_out(0, 2)
+        rows_out("x", 0, 0, "v")
+        wq_transpose(0, 1)
+        wq_scale_out(0, 3)
+        load_wdown(0)
+        wq_scale_out(0, 0)
+        rows_quantise("x", 1)
+        rows_transpose("d", 0, 0, 2, "z")
+        load_wq(1)
+        load_wdown(2)
+        rows_out("x", 2, 1, "v")
+        load_wdown(1)
+        load_rope()
+        wq_widen(1, 0, 0, 1024)
+        rows_quantise("x", 2)
+        wq_scale_out(0, 1)
+        load_wq(2)
+        rows_transpose("d", 3, 0, 0, "q")
+        wq_widen(1, 1, 0, 1024)
         rows_out("d", 0, 0, "s")
-        rows_out("d", 0, 1, "s")
-        rows_tr("d", 1, 0)
-        rows_tr("d", 1, 1)
-        wq_scale(0, 3)
-        rows_out("d", 1, 0, "s")
-        rows_out("d", 1, 1, "v")
-        rows_tr("d", 2, 0)
-        rows_tr("d", 2, 1)
-        wq_quant(0)
-        rows_out("d", 2, 0, "s")
-        rows_out("d", 2, 1, "v")
-        rows_tr("d", 3, 0)
-        rows_tr("d", 3, 1)
-        rows_out("d", 3, 0, "s")
-        rows_out("d", 3, 1, "v")
-        widen2(1, 0)
+        rows_transpose("d", 2, 0, 0, "z")
+        rows_quantise("x", 3)
+        rows_transpose("d", 1, 1, 2, "q")
+        rows_transpose("d", 1, 0, 0, "w")
+        rows_transpose("d", 2, 1, 2, "z")
+        rows_out("d", 3, 0, "v")
+        rope_widen()
+        wq_widen(1, 1, 1024, 2048)
+        rows_out("d", 2, 0, "v")
         biases()
-        wuk_tr(0)
-        wuk_out(0, "s")
-        for g in range(G):
-            rows_quant("d", g, dw, ds)
-        tr(4)
-        lkv_mm(0)
-        wq_scale(1, 0)
-        widen2(1, 1)
-        lkv_mm(1)
-        lkv_out(0)
-        tr(5)
-        wuk_quant(0)
-        wuk_tr(1)
-        wuk_out(1, "s")
-        lkv_mm(2)
-        lkv_out(1)
-        wq_scale(1, 1)
-        tr(6)
-        lkv_mm(3)
-        lkv_out(2)
+        wq_quantise(0)
+        rows_quantise("x", 0)
+        wq_widen(1, 0, 1024, 2048)
+        rows_out("d", 1, 0, "s")
+        load_wuk(2)
+        rows_out("d", 1, 1, "s")
+        load_wq(3)
+        rows_quantise("d", 1)
+        rows_transpose("d", 0, 1, 0, "w")
+        wq_transpose(1, 3)
+        rows_quantise("d", 0)
+        rows_out("d", 2, 1, "v")
+        rows_transpose("d", 3, 1, 2, "q")
+        wq_scale_out(1, 3)
+        rows_out("d", 0, 1, "s")
+        wq_transpose(1, 1)
+        wq_transpose(1, 2, busy=2)
+        wq_widen(2, 0, 0, 1024)
+        rope_transpose()
+        load_wq(6)
+        rows_out("d", 3, 1, "s")
+        wuk_transpose(0)
+        rope_key()
+        rows_quantise("d", 3)
+        rows_quantise("d", 2)
+        wq_scale_out(1, 2)
+        lkv_matmul(3)
+        wuk_out(0, "v")
         lkv_out(3)
-        wuk_quant(1)
-        lkv_quant()
-        q_mm(0, 0)
-        k_mm(0, 0)
-        k_out(0, 0)
-        k_mm(0, 1)
-        k_out(0, 1)
-        q_mm(0, 1)
-
-        def step(j):
-            a = j + 1
-            has_a = a < J
-            p = j - 1
-            has_p = p >= 0
-            ge = "g" if has_a else "v"
-            k_tab(j, 0, "g")
-            k_tab(j, 1, "g")
-            k_rot(j, "g")
-            widen2(j + 2, 0)
-            if has_a and j > 0:
-                wq_scale(a, 0)
-                tr(4 * a + 2)
-            q_tab(j, 0)
-            q_k(j, 0)
-            q_tab(j, 1)
-            q_k(j, 1)
-            q_rot(j, ge)
-            z_even(j, ge)
-            dot(j, ge)
-            dot_rho(j, ge)
-            if has_a:
-                if j > 0:
-                    wq_scale(a, 1)
-                tr(4 * a + 3)
-            if has_p:
-                z_min(p, 0)
-                z_min(p, 1)
-                z_exp(p, 0)
-                z_exp(p, 1)
-            if has_a:
-                k_mm(a, 0)
-            if a + 1 < J:
-                wuk_tr(a + 1)
-                wuk_out(a + 1, "s")
-            widen2(j + 2, 1)
-            if has_a:
-                wq_scale(a, 2)
-                tr(4 * a + 4)
-                wq_scale(a, 3)
-                tr(4 * a + 5)
-            if has_p:
-                for bb in range(2):
-                    z_rcp(p, bb)
-                    z_norm(p, bb)
-            if has_a:
-                wq_quant(a)
-                q_mm(a, 0)
-                k_out(a, 0)
-                k_mm(a, 1)
-                k_out(a, 1)
-                q_mm(a, 1)
-            if a + 1 < J:
-                wuk_quant(a + 1)
-            z_odd(j, "v")
-            z_tr(j, 0)
-            z_tr(j, 1)
+        wuk_quantise(0)
+        wq_widen(2, 1, 0, 1024)
+        lkv_matmul(0)
+        lkv_matmul(1)
+        lkv_out(0)
+        rope_query()
+        load_wuk(3)
+        wq_widen(2, 1, 1024, 2048)
+        wq_scale_out(1, 1)
+        lkv_matmul(2)
+        lkv_out(1)
+        lkv_out(2)
+        wq_transpose(1, 0)
+        lkv_quantise()
+        wuk_transpose(1)
+        wuk_out(1, "s")
+        k_matmul(0, 0)
+        q_matmul(0, 0)
+        load_wq(4)
+        k_bias(0, 0)
+        rope_squares()
+        wq_scale_out(1, 0)
+        load_wuk(1)
+        k_matmul(0, 1)
+        wuk_quantise(1)
+        rope_rho()
+        k_bias(0, 1)
+        load_wq(5)
+        wq_widen(2, 0, 1024, 2048)
+        load_wq(7)
+        wq_quantise(1)
+        wq_transpose(2, 1)
+        wq_transpose(2, 0)
+        q_matmul(0, 1)
 
         for j in range(J):
-            step(j)
-        for bb in range(2):
-            z_min(J - 1, bb)
-            z_exp(J - 1, bb)
-        for bb in range(2):
-            z_rcp(J - 1, bb)
-            z_norm(J - 1, bb)
+            a = j + 2
+            n = j + 1
+            p = j - 1
+            has_a = a < J
+            has_n = n < J
+            has_p = p >= 0
+            last = j == J - 1
+            eng = "g" if has_a else "v"
+            k_table(j, 1)
+            q_times_k(j, 0)
+            q_table(j, 0)
+            if has_a:
+                wq_transpose(a, 2)
+            wq_widen(j + 3, 0)
+            if has_a:
+                wq_scale_out(a, 1)
+            q_times_k(j, 1)
+            if not last:
+                dot(j)
+            if has_a:
+                wq_transpose(a, 3)
+            if has_p:
+                z_min(p, 0)
+            q_table(j, 1)
+            if has_p:
+                z_min(p, 1)
+            k_table(j, 0)
+            if has_a:
+                wq_scale_out(a, 0)
+            wq_widen(j + 3, 1)
+            if has_p:
+                z_exp(p, 0)
+                z_exp(p, 1)
+            if not last:
+                dot_rho(j)
+            if has_a:
+                wq_scale_out(a, 2)
+            if has_n:
+                q_matmul(n, 1)
+                k_matmul(n, 0)
+            if has_a:
+                wuk_transpose(a)
+            k_rotate(j, eng)
+            if not last:
+                q_rotate(j, "g")
+            if last:
+                last_z(j, 0)
+            if has_p:
+                z_reciprocal(p, 0, 2)
+            if last:
+                last_z(j, 1)
+            if has_a:
+                wq_scale_out(a, 3)
+            if not last:
+                z_even(j, eng)
+            if has_n:
+                k_bias(n, 0)
+            if has_a:
+                wuk_out(a, "s")
+            if has_p:
+                z_store(p, 0, "s")
+            if has_n:
+                q_matmul(n, 0)
+            if not last:
+                z_odd(j, "g")
+            if has_a:
+                wuk_quantise(a)
+            if has_n:
+                k_matmul(n, 1)
+                k_bias(n, 1)
+            if not last:
+                z_transpose(j, 0)
+            if has_p:
+                z_store(p, 1, "s")
+            if last:
+                z_transpose(j, 0)
+                z_transpose(j, 1)
+            if has_a:
+                wq_transpose(a + 1, 1)
+                wq_quantise(a)
+            if not last:
+                z_transpose(j, 1)
+            if has_a:
+                wq_transpose(a + 1, 0, busy=2)
+
+        z_min(J - 1, 0)
+        z_exp(J - 1, 0)
+        z_min(J - 1, 1)
+        z_reciprocal(J - 1, 0, 1)
+        z_store(J - 1, 0, "v")
+        z_exp(J - 1, 1)
+        z_reciprocal(J - 1, 1, 2)
+        z_store(J - 1, 1, "v")

from contextlib import ExitStack

import concourse.mybir as mybir
from concourse.masks import make_identity

F32 = mybir.dt.float32
BF16 = mybir.dt.bfloat16
U32 = mybir.dt.uint32
U8 = mybir.dt.uint8
FP8 = mybir.dt.float8_e4m3fn
FP8X4 = mybir.dt.float8_e4m3fn_x4
ALU = mybir.AluOpType
ACT = mybir.ActivationFunctionType
AX = mybir.AxisListType

B, S, DIM, KV, H = 4, 128, 2048, 512, 16
HD = DIM // H
PAIRS = HD // 2
T = B * S
P = 128
G = DIM // 512
J = H // 2
KAPPA = DIM**-0.5

FLOPS = 2 * T * (DIM * KV + DIM * DIM + KV * DIM)


def tile_multilatentattention_pa_kernel(
    tc, x, rope_cos, rope_sin, W_kv_down, b_kv_down, Wq_bytes, Wq_scale, bq, W_uk, b_uk, out
):
    nc = tc.nc
    with ExitStack() as ctx:
        ctx.enter_context(tc.manual_schedule())
        keep = ctx.enter_context(tc.tile_pool(name="keep", bufs=1))
        work = ctx.enter_context(tc.tile_pool(name="work", bufs=2))
        psum = ctx.enter_context(tc.psum_pool(name="psum", bufs=1))
        BANKS = {"w": 3, "q": 2, "z": 2, "k": 1}

        ident = keep.tile([P, P], F32, name="ident")
        make_identity(nc, ident[:])
        warm = keep.tile([P, 1], F32, name="warm")
        nc.vector.memset(warm[:], 0.0)
        nc.scalar.activation(out=warm[:], in_=warm[:], func=ACT.Exp)

        wq_sc = keep.tile([P, G * 4], F32, name="wq_sc")
        nc.sync.dma_start(
            out=wq_sc[:].rearrange("p (g t) -> p g t", t=4),
            in_=Wq_scale.rearrange("o (g p t) -> p (o g) t", p=P, t=4),
        )
        bd_raw = keep.tile([P, 4], BF16, name="bd_raw")
        nc.gpsimd.dma_start(out=bd_raw[:], in_=b_kv_down.rearrange("(p t) -> p t", t=4))
        bqk_raw = keep.tile([P, 2, J, 2], BF16, name="bqk_raw")
        nc.gpsimd.dma_start(out=bqk_raw[:, 0], in_=bq.rearrange("(j p e) -> p j e", p=P, e=2))
        nc.gpsimd.dma_start(out=bqk_raw[:, 1], in_=b_uk.rearrange("(j p e) -> p j e", p=P, e=2))
        cs_raw = keep.tile([P, 2, 2, PAIRS], BF16, name="cs_raw")
        raws = {}
        wq_bytes = {}

        def load_rope():
            for h in range(2):
                nc.sync.dma_start(out=cs_raw[:, 0, h, :], in_=rope_cos)
                nc.sync.dma_start(out=cs_raw[:, 1, h, :], in_=rope_sin)

        def load_x(b):
            raw = work.tile([P, DIM], BF16, name="raw", bufs=8)
            nc.sync.dma_start(out=raw[:], in_=x[b])
            raws["x", b] = raw

        def load_wdown(t):
            raw = work.tile([P, DIM], BF16, name="raw", bufs=8)
            nc.sync.dma_start(out=raw[:], in_=W_kv_down.rearrange("(m t) k -> t m k", t=4)[t])
            raws["d", t] = raw

        def load_wuk(jj):
            raw = work.tile([P, DIM], BF16, name="raw", bufs=8)
            nc.sync.dma_start(
                out=raw[:].rearrange("p (j c) -> p j c", j=2),
                in_=W_uk.rearrange("(j p e) k -> p j (e k)", p=P, e=2)[:, 2 * jj : 2 * jj + 2, :],
            )
            raws["u", jj] = raw

        def load_wq(j, k0=0, k1=DIM):
            if j not in wq_bytes:
                byt = work.tile([P, 2, DIM], U8, name="byt", bufs=4)
                wq_bytes[j] = byt
            nc.sync.dma_start(
                out=wq_bytes[j][:, :, k0:k1],
                in_=Wq_bytes.rearrange("(j p e) k -> j p e k", p=P, e=2)[j][:, :, k0:k1],
            )

        csf = keep.tile([P, 2, P], F32, name="csf")
        tk = keep.tile([P, 2, P], F32, name="tk")
        tq = keep.tile([P, 2, P], F32, name="tq")
        rr = keep.tile([P, 2, P], F32, name="rr")
        rho = keep.tile([P, P], F32, name="rho")
        bd = keep.tile([P, 4], F32, name="bd")
        bqk = keep.tile([P, 2, J, 2], F32, name="bqk")
        tbank = {}

        def rope_widen():
            nc.scalar.copy(csf[:], cs_raw[:].rearrange("p a h i -> p a (h i)"))

        def rope_transpose():
            bank = psum.tile([P, 2, P], F32, name="rope_bank", tag="z", bufs=BANKS["z"])
            for a in range(2):
                nc.tensor.transpose(bank[:, a, :], csf[:, a, :], ident[:])
            tbank[0] = bank

        def rope_key():
            nc.scalar.copy(tk[:], tbank[0][:])

        def rope_query():
            nc.scalar.activation(out=tq[:], in_=tk[:], func=ACT.Copy, scale=-KAPPA)

        def rope_squares():
            nc.gpsimd.tensor_tensor(out=rr[:], in0=tk[:], in1=tq[:], op=ALU.mult)

        def rope_rho():
            nc.gpsimd.tensor_tensor(out=rho[:], in0=rr[:, 0, :], in1=rr[:, 1, :], op=ALU.add)

        def biases():
            nc.scalar.copy(bd[:], bd_raw[:])
            nc.scalar.copy(bqk[:], bqk_raw[:])

        def over_batches(tab):
            return tab.unsqueeze(1).to_broadcast([P, B, S])

        def by_batch(ap):
            return ap.rearrange("p (b s) -> p b s", b=B)

        def copy_out(eng, out_ap, in_ap):
            if eng == "v":
                nc.vector.tensor_copy(out=out_ap, in_=in_ap)
            else:
                nc.scalar.copy(out_ap, in_ap)

        def elementwise(eng, out_ap, a, b, op):
            if eng == "v":
                nc.vector.tensor_tensor(out=out_ap, in0=a, in1=b, op=op)
            else:
                nc.gpsimd.tensor_tensor(out=out_ap, in0=a, in1=b, op=op)

        def keep_busy(bank_ap, n):
            for i in range(n):
                nc.tensor.matmul(bank_ap, lhsT=ident[:], rhs=ident[:], start=True, stop=True)

        xw = keep.tile([P, G, T], U32, name="xw", align_bytes=64)
        xs = keep.tile([P, G, T], U8, name="xs", align_bytes=64)
        dw = keep.tile([P, G, KV], U32, name="dw", align_bytes=64)
        ds = keep.tile([P, G, KV], U8, name="ds", align_bytes=64)
        codes = {"x": (xw, xs), "d": (dw, ds)}
        row_banks = {}
        groups = {}

        def rows_transpose(kind, b, gg, busy, tag):
            words = raws[kind, b][:].bitcast(F32)
            bank = psum.tile([P, 2, 2, P], F32, name="row_bank", tag=tag, bufs=BANKS[tag])
            keep_busy(bank[:, 0, 0, :], busy)
            for g2 in range(2):
                g = 2 * gg + g2
                for u in range(2):
                    nc.tensor.transpose(bank[:, g2, u, :], words[:, 256 * g + u : 256 * (g + 1) : 2], ident[:])
            row_banks[kind, b, gg] = bank

        def rows_out(kind, b, gg, eng):
            if (kind, gg) not in groups:
                grp = work.tile([P, 2, T, 4], BF16, name="grp", bufs=3, align_bytes=64)
                groups[kind, gg] = grp
            dst = groups[kind, gg][:, :, P * b : P * (b + 1), :]
            copy_out(
                eng,
                dst.rearrange("p g n t -> p g (n t)").bitcast(F32).rearrange("p g (n u) -> p g n u", u=2),
                row_banks[kind, b, gg][:].rearrange("p g u n -> p g n u"),
            )

        def rows_quantise(kind, g):
            words, scales = codes[kind]
            nc.vector.quantize_mx(
                out=words[:, g, :].bitcast(FP8X4),
                scales=scales[:, g, :],
                in_=groups[kind, g // 2][:, g % 2].rearrange("p n t -> p (n t)"),
            )

        wides = {}
        wq_banks = {}
        wq_groups = {}
        wq_codes = {}

        def wide_tile(j):
            if j not in wides:
                wide = work.tile([P, 2, DIM], BF16, name="wide", bufs=3)
                wides[j] = wide
            return wides[j]

        def wq_widen(j, e, k0=0, k1=DIM):
            if j < J:
                nc.scalar.copy(wide_tile(j)[:, e, k0:k1], wq_bytes[j][:, e, k0:k1].bitcast(FP8))

        def wq_transpose(j, g, busy=0):
            if j < J:
                bank = psum.tile([P, 2, 256], F32, name="wq_bank", tag="w", bufs=BANKS["w"])
                keep_busy(bank[:, 0, 0:P], busy)
                for e in range(2):
                    words = wides[j][:, e, :].bitcast(F32)
                    for u in range(2):
                        nc.tensor.transpose(
                            bank[:, u, P * e : P * (e + 1)],
                            words[:, 256 * g + u : 256 * (g + 1) : 2],
                            ident[:],
                        )
                wq_banks[j, g] = bank

        def wq_scale_out(j, g):
            if j not in wq_groups:
                wgrp = work.tile([P, G, 256 * 4], BF16, name="wgrp", bufs=2, align_bytes=64)
                wq_groups[j] = wgrp
            nc.vector.tensor_tensor(
                out=wq_groups[j][:, g, :].rearrange("p (n u e) -> p n u e", u=2, e=2),
                in0=wq_banks[j, g][:].bitcast(BF16).rearrange("p u (n e) -> p n u e", e=2),
                in1=wq_sc[:, 4 * g : 4 * g + 4]
                .rearrange("p (u e) -> p u e", e=2)
                .unsqueeze(1)
                .to_broadcast([P, 256, 2, 2]),
                op=ALU.mult,
            )

        def wq_quantise(j):
            wcode = work.tile([P, G * 256], U32, name="wcode", bufs=3, align_bytes=64)
            wscal = work.tile([P, G * 256], U8, name="wscal", bufs=3, align_bytes=64)
            nc.vector.quantize_mx(
                out=wcode[:].bitcast(FP8X4),
                scales=wscal[:],
                in_=wq_groups[j][:].rearrange("p g c -> p (g c)"),
            )
            wq_codes[j] = (wcode, wscal)

        uw = keep.tile([P, J, 2, P], U32, name="uw", align_bytes=64)
        us = keep.tile([P, J, 2, P], U8, name="us", align_bytes=64)
        wuk_banks = {}
        wuk_groups = {}

        def wuk_transpose(j):
            bank = psum.tile([P, 2, 2, P], F32, name="wuk_bank", tag="w", bufs=BANKS["w"])
            words = raws["u", j // 2][:].bitcast(F32).rearrange("p (j e w) -> p j e w", j=2, e=2)
            for e in range(2):
                for u in range(2):
                    nc.tensor.transpose(bank[:, e, u, :], words[:, j % 2, e, u:256:2], ident[:])
            wuk_banks[j] = bank

        def wuk_out(j, eng):
            ugrp = work.tile([P, 2, P, 4], BF16, name="ugrp", bufs=2, align_bytes=64)
            copy_out(
                eng,
                ugrp[:].rearrange("p e n t -> p e (n t)").bitcast(F32).rearrange("p e (n u) -> p e n u", u=2),
                wuk_banks[j][:].rearrange("p e u n -> p e n u"),
            )
            wuk_groups[j] = ugrp

        def wuk_quantise(j):
            nc.vector.quantize_mx(
                out=uw[:, j].rearrange("p e n -> p (e n)").bitcast(FP8X4),
                scales=us[:, j].rearrange("p e n -> p (e n)"),
                in_=wuk_groups[j][:].rearrange("p e n t -> p (e n t)"),
            )

        lg = keep.tile([P, T, 4], BF16, name="lg", align_bytes=64)
        lw = keep.tile([P, T], U32, name="lw", align_bytes=64)
        ls = keep.tile([P, T], U8, name="ls", align_bytes=64)
        lkv_banks = {}

        def lkv_matmul(b):
            bank = psum.tile([P, 4, P], F32, name="lkv_bank", tag="z", bufs=BANKS["z"])
            for t in range(4):
                for g in range(G):
                    nc.tensor.matmul_mx(
                        out=bank[:, t, :],
                        lhsT=dw[:, g, P * t : P * (t + 1)].bitcast(FP8X4),
                        lhsT_scale=ds[:, g, P * t : P * (t + 1)],
                        rhs=xw[:, g, P * b : P * (b + 1)].bitcast(FP8X4),
                        rhs_scale=xs[:, g, P * b : P * (b + 1)],
                        start=(g == 0),
                        stop=(g == G - 1),
                    )
            lkv_banks[b] = bank

        def lkv_out(b):
            nc.vector.tensor_tensor(
                out=lg[:, P * b : P * (b + 1), :],
                in0=lkv_banks[b][:].rearrange("p t n -> p n t"),
                in1=bd[:].unsqueeze(1).to_broadcast([P, P, 4]),
                op=ALU.add,
            )

        def lkv_quantise():
            nc.vector.quantize_mx(
                out=lw[:].bitcast(FP8X4), scales=ls[:], in_=lg[:].rearrange("p n t -> p (n t)")
            )

        k_banks = {}
        q_banks = {}
        kts = {}
        kcs = {}
        qts = {}
        pts = {}
        dot_banks = {}
        zes = {}
        zos = {}

        def k_matmul(j, e):
            bank = psum.tile([P, T], F32, name="k_bank", tag="k", bufs=BANKS["k"])
            nc.tensor.matmul_mx(
                out=bank[:],
                lhsT=uw[:, j, e, :].bitcast(FP8X4),
                lhsT_scale=us[:, j, e, :],
                rhs=lw[:].bitcast(FP8X4),
                rhs_scale=ls[:],
                start=True,
                stop=True,
            )
            k_banks[j, e] = bank

        def k_bias(j, e):
            kt = work.tile([P, T], F32, name="kt%d" % e, bufs=2)
            nc.scalar.activation(
                out=kt[:], in_=k_banks[j, e][:], func=ACT.Identity, bias=bqk[:, 1, j, e : e + 1], scale=1.0
            )
            kts[j, e] = kt

        def q_matmul(j, e):
            wcode, wscal = wq_codes[j]
            bank = psum.tile([P, T], F32, name="q_bank", tag="q", bufs=BANKS["q"])
            for g in range(G):
                c = slice(256 * g + P * e, 256 * g + P * (e + 1))
                nc.tensor.matmul_mx(
                    out=bank[:],
                    lhsT=wcode[:, c].bitcast(FP8X4),
                    lhsT_scale=wscal[:, c],
                    rhs=xw[:, g, :].bitcast(FP8X4),
                    rhs_scale=xs[:, g, :],
                    start=(g == 0),
                    stop=(g == G - 1),
                )
            q_banks[j, e] = bank

        def q_table(j, e):
            qt = work.tile([P, T], F32, name="qt%d" % e, bufs=2)
            nc.vector.scalar_tensor_tensor(
                out=by_batch(qt[:]), in0=by_batch(q_banks[j, e][:]), scalar=bqk[:, 0, j, e : e + 1],
                in1=over_batches(tq[:, e, :]), op0=ALU.add, op1=ALU.mult,
            )
            qts[j, e] = qt

        def q_times_k(j, e):
            pt = work.tile([P, T], F32, name="pt%d" % e, bufs=2)
            nc.vector.scalar_tensor_tensor(
                out=pt[:], in0=q_banks[j, e][:], scalar=bqk[:, 0, j, e : e + 1], in1=kts[j, e][:],
                op0=ALU.add, op1=ALU.mult,
            )
            pts[j, e] = pt

        def k_table(j, e):
            kc = work.tile([P, T], F32, name="kc%d" % e, bufs=2)
            elementwise("g", by_batch(kc[:]), by_batch(kts[j, e][:]), over_batches(tk[:, e, :]), ALU.mult)
            kcs[j, e] = kc

        def k_rotate(j, eng):
            elementwise(eng, kcs[j, 0][:], kcs[j, 0][:], kcs[j, 1][:], ALU.subtract)

        def q_rotate(j, eng):
            elementwise(eng, qts[j, 0][:], qts[j, 0][:], qts[j, 1][:], ALU.subtract)

        def dot(j):
            bank = psum.tile([P, T], F32, name="dot_bank", tag="k", bufs=BANKS["k"])
            for e in range(2):
                nc.tensor.matmul(bank[:], lhsT=ident[:], rhs=pts[j, e][:], start=(e == 0), stop=(e == 1))
            dot_banks[j] = bank

        def dot_rho(j):
            nc.vector.tensor_tensor(
                out=by_batch(pts[j, 0][:]), in0=by_batch(dot_banks[j][:]), in1=over_batches(rho[:]), op=ALU.mult
            )

        def z_even(j, eng):
            ze = work.tile([P, T], F32, name="ze", bufs=2)
            elementwise(eng, ze[:], qts[j, 0][:], kcs[j, 0][:], ALU.mult)
            zes[j] = ze

        def z_odd(j, eng):
            zo = work.tile([P, T], F32, name="zo", bufs=2)
            elementwise(eng, zo[:], pts[j, 0][:], zes[j][:], ALU.subtract)
            zos[j] = zo

        def last_z(j, bb):
            c = slice(2 * S * bb, 2 * S * (bb + 1))
            if bb == 0:
                ze = work.tile([P, T], F32, name="ze", bufs=2)
                zo = work.tile([P, T], F32, name="zo", bufs=2)
                zes[j] = ze
                zos[j] = zo
            ze = zes[j]
            zo = zos[j]
            qc = qts[j, 0][:, c]
            pa = pts[j, 0][:, c]
            pa2 = pa.rearrange("p (b s) -> p b s", b=2)
            nc.vector.tensor_tensor(out=qc, in0=qc, in1=qts[j, 1][:, c], op=ALU.subtract)
            nc.vector.tensor_tensor(out=pa, in0=pa, in1=pts[j, 1][:, c], op=ALU.add)
            nc.vector.tensor_tensor(out=ze[:, c], in0=qc, in1=kcs[j, 0][:, c], op=ALU.mult)
            nc.vector.tensor_tensor(
                out=pa2, in0=pa2, in1=rho[:].unsqueeze(1).to_broadcast([P, 2, S]), op=ALU.mult
            )
            nc.vector.tensor_tensor(out=zo[:, c], in0=pa, in1=ze[:, c], op=ALU.subtract)

        z_banks = {}
        minima = {}
        sums = {}
        reciprocals = {}
        exps = {}

        def z_transpose(j, bb):
            tag = "w" if j == J - 1 else "z"
            bank = psum.tile([P, 2, 2, P], F32, name="z_bank", tag=tag, bufs=BANKS[tag])
            for e, zz in ((0, zes[j]), (1, zos[j])):
                for b in range(2):
                    c = slice(P * (2 * bb + b), P * (2 * bb + b + 1))
                    nc.tensor.transpose(bank[:, b, e, :], zz[:, c], ident[:])
            z_banks[j, bb] = bank

        def z_min(j, bb):
            nm = work.tile([P, 2, 2], F32, name="nm", bufs=4)
            nc.vector.tensor_reduce(
                out=nm[:],
                in_=z_banks[j, bb][:].rearrange("p b e (h i) -> p b h e i", h=2),
                axis=AX.XY,
                op=ALU.min,
            )
            minima[j, bb] = nm

        def z_exp(j, bb):
            et = work.tile([P, 2, 2, HD], F32, name="et", bufs=4)
            if j not in sums:
                sm = work.tile([P, 2, 2, 2], F32, name="sm", bufs=2)
                sums[j] = sm
            for b in range(2):
                for h in range(2):
                    nc.scalar.activation(
                        out=et[:, b, h, :].rearrange("p (i e) -> p i e", e=2),
                        in_=z_banks[j, bb][:, b, :, PAIRS * h : PAIRS * (h + 1)].rearrange("p e i -> p i e"),
                        func=ACT.Exp,
                        bias=minima[j, bb][:, b, h : h + 1],
                        scale=-1.0,
                        accum_out=sums[j][:, bb, b, h : h + 1],
                    )
            exps[j, bb] = et

        def z_reciprocal(j, b0, b1):
            if j not in reciprocals:
                rs = work.tile([P, 2, 2, 2], F32, name="rs", bufs=2)
                reciprocals[j] = rs
            nc.vector.reciprocal(out=reciprocals[j][:, b0:b1], in_=sums[j][:, b0:b1])

        def z_store(j, bb, eng):
            et = exps[j, bb]
            for b in range(2):
                for h in range(2):
                    r = reciprocals[j][:, bb, b, h : h + 1]
                    if eng == "v":
                        nc.vector.tensor_scalar(
                            out=et[:, b, h, :], in0=et[:, b, h, :], scalar1=r, scalar2=None, op0=ALU.mult
                        )
                    else:
                        nc.scalar.activation(out=et[:, b, h, :], in_=et[:, b, h, :], func=ACT.Copy, scale=r)
            for b in range(2):
                nc.sync.dma_start(
                    out=out[2 * bb + b, 2 * j : 2 * j + 2].rearrange("h s d -> s h d"), in_=et[:, b]
                )

        load_x(3)
        load_x(1)
        load_wq(0, 1024, 2048)
        rows_transpose("x", 3, 0, 3, "w")
        wq_widen(0, 0, 1024, 2048)
        rows_transpose("x", 1, 0, 2, "q")
        load_x(0)
        load_wdown(3)
        wq_widen(0, 1, 1024, 2048)
        rows_out("x", 1, 0, "v")
        load_wq(0, 0, 1024)
        wq_widen(0, 0, 0, 1024)
        rows_transpose("x", 3, 1, 0, "q")
        load_wuk(0)
        rows_transpose("x", 1, 1, 2, "w")
        rows_out("x", 3, 1, "v")
        rows_transpose("x", 0, 1, 0, "q")
        rows_out("x", 1, 1, "s")
        wq_transpose(0, 2, busy=2)
        rows_out("x", 3, 0, "v")
        load_x(2)
        wq_transpose(0, 3)
        rows_out("x", 0, 1, "v")
        wq_widen(0, 1, 0, 1024)
        rows_transpose("x", 0, 0, 0, "q")
        wq_transpose(0, 0, busy=2)
        rows_transpose("x", 2, 0, 0, "z")
        rows_transpose("x", 2, 1, 2, "q")
        rows_out("x", 2, 0, "s")
        wq_scale_out(0, 2)
        rows_out("x", 0, 0, "v")
        wq_transpose(0, 1)
        wq_scale_out(0, 3)
        load_wdown(0)
        wq_scale_out(0, 0)
        rows_quantise("x", 1)
        rows_transpose("d", 0, 0, 2, "z")
        load_wq(1)
        load_wdown(2)
        rows_out("x", 2, 1, "v")
        load_wdown(1)
        load_rope()
        wq_widen(1, 0, 0, 1024)
        rows_quantise("x", 2)
        wq_scale_out(0, 1)
        load_wq(2)
        rows_transpose("d", 3, 0, 0, "q")
        wq_widen(1, 1, 0, 1024)
        rows_out("d", 0, 0, "s")
        rows_transpose("d", 2, 0, 0, "z")
        rows_quantise("x", 3)
        rows_transpose("d", 1, 1, 2, "q")
        rows_transpose("d", 1, 0, 0, "w")
        rows_transpose("d", 2, 1, 2, "z")
        rows_out("d", 3, 0, "v")
        rope_widen()
        wq_widen(1, 1, 1024, 2048)
        rows_out("d", 2, 0, "v")
        biases()
        wq_quantise(0)
        rows_quantise("x", 0)
        wq_widen(1, 0, 1024, 2048)
        rows_out("d", 1, 0, "s")
        load_wuk(2)
        rows_out("d", 1, 1, "s")
        load_wq(3)
        rows_quantise("d", 1)
        rows_transpose("d", 0, 1, 0, "w")
        wq_transpose(1, 3)
        rows_quantise("d", 0)
        rows_out("d", 2, 1, "v")
        rows_transpose("d", 3, 1, 2, "q")
        wq_scale_out(1, 3)
        rows_out("d", 0, 1, "s")
        wq_transpose(1, 1)
        wq_transpose(1, 2, busy=2)
        wq_widen(2, 0, 0, 1024)
        rope_transpose()
        load_wq(6)
        rows_out("d", 3, 1, "s")
        wuk_transpose(0)
        rope_key()
        rows_quantise("d", 3)
        rows_quantise("d", 2)
        wq_scale_out(1, 2)
        lkv_matmul(3)
        wuk_out(0, "v")
        lkv_out(3)
        wuk_quantise(0)
        wq_widen(2, 1, 0, 1024)
        lkv_matmul(0)
        lkv_matmul(1)
        lkv_out(0)
        rope_query()
        load_wuk(3)
        wq_widen(2, 1, 1024, 2048)
        wq_scale_out(1, 1)
        lkv_matmul(2)
        lkv_out(1)
        lkv_out(2)
        wq_transpose(1, 0)
        lkv_quantise()
        wuk_transpose(1)
        wuk_out(1, "s")
        k_matmul(0, 0)
        q_matmul(0, 0)
        load_wq(4)
        k_bias(0, 0)
        rope_squares()
        wq_scale_out(1, 0)
        load_wuk(1)
        k_matmul(0, 1)
        wuk_quantise(1)
        rope_rho()
        k_bias(0, 1)
        load_wq(5)
        wq_widen(2, 0, 1024, 2048)
        load_wq(7)
        wq_quantise(1)
        wq_transpose(2, 1)
        wq_transpose(2, 0)
        q_matmul(0, 1)

        for j in range(J):
            a = j + 2
            n = j + 1
            p = j - 1
            has_a = a < J
            has_n = n < J
            has_p = p >= 0
            last = j == J - 1
            eng = "g" if has_a else "v"
            k_table(j, 1)
            q_times_k(j, 0)
            q_table(j, 0)
            if has_a:
                wq_transpose(a, 2)
            wq_widen(j + 3, 0)
            if has_a:
                wq_scale_out(a, 1)
            q_times_k(j, 1)
            if not last:
                dot(j)
            if has_a:
                wq_transpose(a, 3)
            if has_p:
                z_min(p, 0)
            q_table(j, 1)
            if has_p:
                z_min(p, 1)
            k_table(j, 0)
            if has_a:
                wq_scale_out(a, 0)
            wq_widen(j + 3, 1)
            if has_p:
                z_exp(p, 0)
                z_exp(p, 1)
            if not last:
                dot_rho(j)
            if has_a:
                wq_scale_out(a, 2)
            if has_n:
                q_matmul(n, 1)
                k_matmul(n, 0)
            if has_a:
                wuk_transpose(a)
            k_rotate(j, eng)
            if not last:
                q_rotate(j, "g")
            if last:
                last_z(j, 0)
            if has_p:
                z_reciprocal(p, 0, 2)
            if last:
                last_z(j, 1)
            if has_a:
                wq_scale_out(a, 3)
            if not last:
                z_even(j, eng)
            if has_n:
                k_bias(n, 0)
            if has_a:
                wuk_out(a, "s")
            if has_p:
                z_store(p, 0, "s")
            if has_n:
                q_matmul(n, 0)
            if not last:
                z_odd(j, "g")
            if has_a:
                wuk_quantise(a)
            if has_n:
                k_matmul(n, 1)
                k_bias(n, 1)
            if not last:
                z_transpose(j, 0)
            if has_p:
                z_store(p, 1, "s")
            if last:
                z_transpose(j, 0)
                z_transpose(j, 1)
            if has_a:
                wq_transpose(a + 1, 1)
                wq_quantise(a)
            if not last:
                z_transpose(j, 1)
            if has_a:
                wq_transpose(a + 1, 0, busy=2)

        z_min(J - 1, 0)
        z_exp(J - 1, 0)
        z_min(J - 1, 1)
        z_reciprocal(J - 1, 0, 1)
        z_store(J - 1, 0, "v")
        z_exp(J - 1, 1)
        z_reciprocal(J - 1, 1, 2)
        z_store(J - 1, 1, "v")
